import numpy as np
import ml_dtypes


def mxq(x, axis, fmt="e4m3"):
    dtype, down = {"e4m3": (ml_dtypes.float8_e4m3fn, 7), "e5m2": (ml_dtypes.float8_e5m2, 14)}[fmt]
    v = np.moveaxis(np.asarray(x, np.float32).astype(ml_dtypes.bfloat16).astype(np.float64), axis, -1)
    blocks = v.reshape(v.shape[:-1] + (-1, 32))
    amax = np.abs(blocks).max(-1, keepdims=True)
    byte = np.maximum(np.where(amax > 0, np.frexp(amax)[1] - 1 + 127, 0) - down, 1)
    scale = np.exp2(byte - 127.0)
    codes = (blocks / scale).astype(np.float32).astype(dtype).astype(np.float64)
    return np.moveaxis((codes * scale).reshape(v.shape), -1, axis)


WIDE = False


def mx_kscale(k):
    if not WIDE:
        return np.ones(k)
    levels = np.array([10, -10, 5, -5, 0])
    if k % 512:
        return np.exp2(np.random.permutation(np.resize(levels, k // 32))).repeat(32)
    a = np.empty((k // 512, 16))
    for p in range(k // 512):
        a[p, :8] = np.random.permutation(np.resize(levels, 8))
        for g in range(8):
            far = levels[np.abs(levels - a[p, g]) >= 10]
            a[p, g + 8] = far[np.random.randint(len(far))]
    return np.exp2(a.ravel()).repeat(32)


BF16 = ml_dtypes.bfloat16


def bf(x):
    return np.asarray(x, np.float32).astype(BF16)


def f64(x):
    return np.asarray(x).astype(np.float64)


B, S, E, H, DH, F = 4, 128, 1024, 8, 128, 4096
HD = H * DH
EPS = 1e-6
ERF_CLIP = 6.0
ERF_TERMS = 100


def layer_norm(x, g, b):
    m = x.mean(-1, keepdims=True)
    v = np.square(x - m).mean(-1, keepdims=True)
    return (x - m) * (1.0 / np.sqrt(v + EPS)) * g + b


def erf(v):
    a = np.clip(v, -ERF_CLIP, ERF_CLIP)
    a2 = 2.0 * a * a
    term = a.copy()
    tot = a.copy()
    for n in range(1, ERF_TERMS):
        term = term * a2 / (2.0 * n + 1.0)
        tot = tot + term
    return 2.0 / np.sqrt(np.pi) * np.exp(-a * a) * tot


def gelu(v):
    return 0.5 * v * (1.0 + erf(v / np.sqrt(2.0)))


def setup_inputs():
    s = mx_kscale(HD).reshape(H, DH)
    t = mx_kscale(E)
    return {"h_attn": bf(0.35 * np.random.standard_normal((B, S, H, DH)) * s),
            "Wo": bf((np.random.standard_normal((H, DH, E)) + 0.5 * np.random.standard_normal((H, DH, 1))) / np.sqrt(HD) / s[:, :, None]),
            "gamma2": bf((1.0 + 0.1 * np.random.standard_normal(E)) * t),
            "beta2": bf(0.1 * np.random.standard_normal(E) * t),
            "Wg": bf(np.random.standard_normal((E, F)) / np.sqrt(E) / t[:, None]),
            "Wu": bf(np.random.standard_normal((E, F)) / np.sqrt(E) / t[:, None])}


def reference(h_attn, Wo, gamma2, beta2, Wg, Wu):
    attn_out = mxq(f64(h_attn).reshape(B, S, HD), 2, "e4m3") @ mxq(f64(Wo).reshape(HD, E), 0, "e4m3")
    z = layer_norm(attn_out, f64(gamma2), f64(beta2))
    zq = mxq(z, 2, "e4m3")
    gate = gelu(zq @ mxq(f64(Wg), 0, "e4m3"))
    return gate * (zq @ mxq(f64(Wu), 0, "e4m3"))

@@ -1,0 +1,346 @@
+from contextlib import ExitStack
+
+import concourse.mybir as mybir
+from concourse.masks import make_identity
+
+F32 = mybir.dt.float32
+BF16 = mybir.dt.bfloat16
+U32 = mybir.dt.uint32
+U8 = mybir.dt.uint8
+FP8X4 = mybir.dt.float8_e4m3fn_x4
+ACT = mybir.ActivationFunctionType
+ALU = mybir.AluOpType
+
+P = 128
+PACK = 4
+K_PASS = P * PACK
+TOKENS = 512
+TOK_TILES = TOKENS // P
+E = 1024
+F = 4096
+PASSES = E // K_PASS
+N_TILE = 512
+CHUNK = 1024
+TILES_PER_CHUNK = CHUNK // N_TILE
+F_TILES = F // N_TILE
+E_BLOCKS = E // P
+RUN = 4
+EPS = 1e-6
+GB_PITCH = 16
+RAW_BUFS = 5
+GATE = 0
+UP = 1
+GPSIMD_COLS = 256
+FIRST_SHARED_TILE = 3
+
+FLOPS = 2 * TOKENS * E * (E + 2 * F)
+
+
+def regroup(copy, grouped, rows):
+    copy(
+        out=grouped.rearrange("p (c i t) -> p c t i", i=RUN, t=PACK),
+        in_=rows.rearrange("p t (c i) -> p c t i", i=RUN),
+    )
+
+
+def tile_selfdecoderblock_pb_kernel(tc, h_attn, Wo, gamma2, beta2, Wg, Wu, out):
+    nc = tc.nc
+    h_rows_dram = h_attn.rearrange("b s h d -> b s (h d)")
+    wo_dram = Wo.rearrange("h d e -> (h d) e")
+    chunk_order = [(w, c) for c in range(F // CHUNK) for w in (Wg, Wu)]
+
+    with ExitStack() as ctx:
+        ctx.enter_context(tc.manual_schedule())
+        keep = ctx.enter_context(tc.tile_pool(name="keep", bufs=1))
+        raw_pool = ctx.enter_context(tc.tile_pool(name="raw", bufs=RAW_BUFS))
+        stage = ctx.enter_context(tc.tile_pool(name="stage", bufs=10))
+        weights = ctx.enter_context(tc.tile_pool(name="weights", bufs=8))
+        psum = ctx.enter_context(tc.psum_pool(name="psum", bufs=8))
+
+        def bank(shape, dtype):
+            return psum.tile(shape, dtype, name="bank")
+
+        def load_wo():
+            raw = raw_pool.tile([P, PASSES, PACK, CHUNK], BF16, name="raw")
+            for g in range(PASSES):
+                nc.sync.dma_start(
+                    out=raw[:, g],
+                    in_=wo_dram[g * K_PASS : (g + 1) * K_PASS, :].rearrange("(p t) n -> p t n", t=PACK),
+                )
+            return raw
+
+        raws = []
+
+        def load_chunks(count):
+            for w, c in chunk_order[len(raws) : count]:
+                raw = raw_pool.tile([P, PASSES, PACK, CHUNK], BF16, name="raw")
+                for g in range(PASSES):
+                    nc.sync.dma_start(
+                        out=raw[:, g],
+                        in_=w[g * K_PASS : (g + 1) * K_PASS, c * CHUNK : (c + 1) * CHUNK].rearrange(
+                            "(p t) n -> p t n", t=PACK
+                        ),
+                    )
+                raws.append(raw)
+
+        def copy_unit(copy, raw, g, tile_in_chunk):
+            grouped = stage.tile([P, N_TILE * PACK], BF16, name="grouped", align_bytes=64)
+            regroup(copy, grouped[:], raw[:, g, :, tile_in_chunk * N_TILE : (tile_in_chunk + 1) * N_TILE])
+            return grouped
+
+        def quantise_unit(grouped, operand, g, cols):
+            codes, scales = operand
+            nc.vector.quantize_mx(out=codes[:, g, cols].bitcast(FP8X4), scales=scales[:, g, cols], in_=grouped[:])
+
+        def product(acc, left, left_cols, right, right_cols, g):
+            nc.tensor.matmul_mx(
+                out=acc,
+                lhsT=left[0][:, g, left_cols].bitcast(FP8X4),
+                lhsT_scale=left[1][:, g, left_cols],
+                rhs=right[0][:, g, right_cols].bitcast(FP8X4),
+                rhs_scale=right[1][:, g, right_cols],
+                start=(g == 0),
+                stop=(g == PASSES - 1),
+            )
+
+        def tokens(m):
+            return slice(m * P, (m + 1) * P)
+
+        pieces = {}
+        moving = {}
+
+        def copy_weight_piece(copy, grouped, b, j, g, first, width):
+            raw = raws[2 * (j // TILES_PER_CHUNK) + b]
+            start = (j % TILES_PER_CHUNK) * N_TILE + first
+            regroup(copy, grouped[:], raw[:, g, :, start : start + width])
+            pieces[b, j] = pieces.get((b, j), []) + [(grouped, g, first, width)]
+
+        def copy_weight_unit(b, j, g):
+            copy = nc.scalar.copy if g == 0 else nc.vector.tensor_copy
+            shared = b == UP and g == 1 and j >= FIRST_SHARED_TILE
+            width = N_TILE - GPSIMD_COLS if shared else N_TILE
+            grouped = stage.tile([P, width * PACK], BF16, name="grouped", align_bytes=64)
+            copy_weight_piece(copy, grouped, b, j, g, 0, width)
+
+        def gpsimd_copy(out, in_):
+            nc.gpsimd.tensor_scalar(out=out, in0=in_, scalar1=1.0, scalar2=0.0, op0=ALU.mult, op1=ALU.add)
+
+        def copy_gpsimd_share(j):
+            grouped = stage.tile([P, GPSIMD_COLS * PACK], BF16, name="grouped_by_gpsimd", bufs=1, align_bytes=64)
+            copy_weight_piece(gpsimd_copy, grouped, UP, j, 1, N_TILE - GPSIMD_COLS, GPSIMD_COLS)
+
+        def quantise_weight_tile(b, j):
+            moving[b, j] = (
+                weights.tile([P, PASSES, N_TILE], U32, name="codes", align_bytes=64),
+                weights.tile([P, PASSES, N_TILE], U8, name="scales", align_bytes=64),
+            )
+            for grouped, g, first, width in pieces[b, j]:
+                quantise_unit(grouped, moving[b, j], g, slice(first, first + width))
+
+        ident_f32 = keep.tile([P, P], F32, name="ident_f32")
+        make_identity(nc, ident_f32[:])
+        eps = keep.tile([P, 1], F32, name="eps")
+        nc.vector.memset(eps[:], EPS)
+        warm = keep.tile([P, 2], F32, name="warm")
+        z = (
+            keep.tile([P, PASSES, TOKENS], U32, name="z_codes", align_bytes=64),
+            keep.tile([P, PASSES, TOKENS], U8, name="z_scales", align_bytes=64),
+        )
+
+        with tc.tile_pool(name="early", bufs=1) as early:
+            wo_raw = load_wo()
+            h_rows = []
+            for m in range(TOK_TILES):
+                rows = early.tile([P, E], BF16, name="h_rows%d" % m)
+                nc.sync.dma_start(out=rows[:], in_=h_rows_dram[m])
+                h_rows.append(rows)
+            gb_rows = early.tile([P, 2, PASSES, GB_PITCH], BF16, name="gb_rows")
+            for i, vec in enumerate((gamma2, beta2)):
+                nc.sync.dma_start(
+                    out=gb_rows[:, i, :, 0:PACK], in_=vec.rearrange("(g p t) -> p g t", g=PASSES, t=PACK)
+                )
+            load_chunks(RAW_BUFS - 1)
+            nc.scalar.activation(out=warm[:, 0:1], in_=eps[:], func=ACT.Sqrt)
+
+            wo = (
+                early.tile([P, PASSES, E], U32, name="wo_codes", align_bytes=64),
+                early.tile([P, PASSES, E], U8, name="wo_scales", align_bytes=64),
+            )
+            wo_grouped = {}
+            for g in range(PASSES):
+                wo_grouped[g, 0] = copy_unit(nc.vector.tensor_copy, wo_raw, g, 0)
+                wo_grouped[g, 1] = copy_unit(nc.scalar.copy, wo_raw, g, 1)
+                if g > 0:
+                    quantise_unit(wo_grouped[g - 1, 1], wo, g - 1, slice(N_TILE, 2 * N_TILE))
+                quantise_unit(wo_grouped[g, 0], wo, g, slice(0, N_TILE))
+            quantise_unit(wo_grouped[PASSES - 1, 1], wo, PASSES - 1, slice(N_TILE, 2 * N_TILE))
+            load_chunks(RAW_BUFS)
+
+            h = (
+                early.tile([P, PASSES, TOKENS], U32, name="h_codes", align_bytes=64),
+                early.tile([P, PASSES, TOKENS], U8, name="h_scales", align_bytes=64),
+            )
+            h_grouped = []
+            for m in range(TOK_TILES):
+                words = bank([P, PASSES * 2, P], F32)
+                for q in range(PASSES * 2):
+                    nc.tensor.transpose(
+                        words[:, q, :],
+                        h_rows[m][:].bitcast(F32)[:, (q // 2) * 2 * P + q % 2 : (q // 2 + 1) * 2 * P : 2],
+                        ident_f32[:],
+                    )
+                grouped = early.tile([P, PASSES, P * PACK], BF16, name="h_grouped%d" % m, align_bytes=64)
+                nc.scalar.copy(
+                    out=grouped[:].bitcast(F32).rearrange("p g (r u) -> p g r u", u=2),
+                    in_=words[:].rearrange("p (g u) r -> p g r u", u=2),
+                )
+                h_grouped.append(grouped)
+
+            a = {}
+            for m in range(TOK_TILES):
+                for g in range(PASSES):
+                    nc.vector.quantize_mx(
+                        out=h[0][:, g, tokens(m)].bitcast(FP8X4), scales=h[1][:, g, tokens(m)], in_=h_grouped[m][:, g, :]
+                    )
+                for n in range(TILES_PER_CHUNK):
+                    a[m, n] = bank([P, N_TILE], F32)
+                    for g in range(PASSES):
+                        product(a[m, n][:], h, tokens(m), wo, slice(n * N_TILE, (n + 1) * N_TILE), g)
+
+            stats = early.tile([P, TOK_TILES, TILES_PER_CHUNK, 6], F32, name="stats")
+            mean_var = early.tile([P, TOK_TILES, 2], F32, name="mean_var")
+            std = early.tile([P, TOK_TILES], F32, name="std")
+            rstd = early.tile([P, TOK_TILES], F32, name="rstd")
+            shift = early.tile([P, TOK_TILES], F32, name="shift")
+            normed = [early.tile([P, E], F32, name="normed%d" % m) for m in range(TOK_TILES)]
+
+            gain_bias = early.tile([P, 2 * E_BLOCKS], F32, name="gain_bias")
+            nc.vector.tensor_copy(
+                out=gain_bias[:].rearrange("p (i g t) -> p i g t", i=2, t=PACK), in_=gb_rows[:, :, :, 0:PACK]
+            )
+            copy_weight_unit(GATE, 0, 0)
+            copy_weight_unit(GATE, 1, 0)
+            copy_weight_unit(UP, 0, 0)
+            for m in range(TOK_TILES):
+                for n in range(TILES_PER_CHUNK):
+                    nc.vector.bn_stats(out=stats[:, m, n, :], in_=a[m, n][:])
+                nc.vector.bn_aggr(out=mean_var[:, m, :], in_=stats[:, m].rearrange("p n s -> p (n s)"))
+            copy_weight_unit(GATE, 0, 1)
+            nc.scalar.activation(out=std[:], in_=mean_var[:, :, 1], func=ACT.Sqrt, bias=eps[:], scale=1.0)
+            nc.vector.reciprocal(out=rstd[:], in_=std[:])
+            nc.vector.scalar_tensor_tensor(
+                out=shift[:], in0=mean_var[:, :, 0], scalar=-1.0, in1=rstd[:], op0=ALU.mult, op1=ALU.mult
+            )
+
+            def normalise(m):
+                for n in range(TILES_PER_CHUNK):
+                    nc.scalar.activation(
+                        out=normed[m][:, n * N_TILE : (n + 1) * N_TILE].rearrange("p (t q) -> p t q", t=PACK),
+                        in_=a[m, n][:].rearrange("p (q t) -> p t q", t=PACK),
+                        func=ACT.Identity,
+                        scale=rstd[:, m : m + 1],
+                        bias=shift[:, m : m + 1],
+                    )
+
+            z_planes = early.tile([P, E_BLOCKS, TOKENS], BF16, name="z_planes")
+
+            def half_tokens(q):
+                return slice(q * 2 * P, (q + 1) * 2 * P)
+
+            def flip(q):
+                for first_block in range(0, E_BLOCKS, 2):
+                    flipped = bank([P, 2, 2 * P], F32)
+                    for i in range(2):
+                        r = first_block + i
+                        for tile_in_half in range(2):
+                            nc.tensor.transpose(
+                                flipped[:, i, tokens(tile_in_half)],
+                                normed[2 * q + tile_in_half][:, r * P : (r + 1) * P],
+                                ident_f32[:],
+                            )
+                    for i in range(2):
+                        r = first_block + i
+                        gain = gain_bias[:, r : r + 1]
+                        bias = gain_bias[:, E_BLOCKS + r : E_BLOCKS + r + 1]
+                        if q == 0:
+                            nc.vector.tensor_scalar(
+                                out=z_planes[:, r, half_tokens(q)],
+                                in0=flipped[:, i, :],
+                                scalar1=gain,
+                                scalar2=bias,
+                                op0=ALU.mult,
+                                op1=ALU.add,
+                            )
+                        else:
+                            nc.scalar.activation(
+                                out=z_planes[:, r, half_tokens(q)],
+                                in_=flipped[:, i, :],
+                                func=ACT.Identity,
+                                scale=gain,
+                                bias=bias,
+                            )
+
+            copy_weight_unit(GATE, 1, 1)
+            quantise_weight_tile(GATE, 0)
+            quantise_weight_tile(GATE, 1)
+            normalise(0)
+            normalise(1)
+            flip(0)
+            normalise(2)
+            normalise(3)
+            flip(1)
+            nc.scalar.activation(out=warm[:, 1:2], in_=z_planes[:, E_BLOCKS - 1, TOKENS - 1 : TOKENS], func=ACT.Gelu)
+            for q in range(2):
+                z_grouped = []
+                for g in range(PASSES):
+                    grouped = early.tile([P, 2 * P * PACK], BF16, name="z_grouped%d%d" % (q, g), align_bytes=64)
+                    regroup(nc.vector.tensor_copy, grouped[:], z_planes[:, g * PACK : (g + 1) * PACK, half_tokens(q)])
+                    z_grouped.append(grouped)
+                copy_weight_unit(UP, q, 1)
+                for g in range(PASSES):
+                    quantise_unit(z_grouped[g], z, g, half_tokens(q))
+
+        late = ctx.enter_context(tc.tile_pool(name="late", bufs=1, reuse_waits="tile"))
+        gates = {}
+
+        def gate_branch(j):
+            for m in range(TOK_TILES):
+                acc = bank([P, N_TILE], F32)
+                for g in range(PASSES):
+                    product(acc[:], z, tokens(m), moving[GATE, j], slice(0, N_TILE), g)
+                gates[j, m] = late.tile([P, N_TILE], F32, name="gate", bufs=2 * TOK_TILES)
+                nc.scalar.activation(out=gates[j, m][:], in_=acc[:], func=ACT.Gelu)
+
+        def up_branch(j):
+            for m in range(TOK_TILES):
+                acc = bank([P, N_TILE], F32)
+                for g in range(PASSES):
+                    product(acc[:], z, tokens(m), moving[UP, j], slice(0, N_TILE), g)
+                result = late.tile([P, N_TILE], F32, name="result", bufs=2 * TOK_TILES)
+                nc.vector.tensor_tensor(out=result[:], in0=gates[j, m][:], in1=acc[:], op=ALU.mult)
+                nc.sync.dma_start(out=out[m, :, j * N_TILE : (j + 1) * N_TILE], in_=result[:])
+
+        def copy_weight_tiles(j):
+            for b in (GATE, UP):
+                for g in range(PASSES):
+                    copy_weight_unit(b, j, g)
+            if j % TILES_PER_CHUNK == TILES_PER_CHUNK - 1:
+                load_chunks(RAW_BUFS + j + 1)
+
+        copy_weight_unit(UP, 1, 0)
+        load_chunks(RAW_BUFS + 2)
+        quantise_weight_tile(UP, 0)
+        gate_branch(0)
+        copy_weight_tiles(2)
+        quantise_weight_tile(UP, 1)
+        for j in range(F_TILES):
+            up_branch(j)
+            if FIRST_SHARED_TILE <= j + 2 < F_TILES:
+                copy_gpsimd_share(j + 2)
+            if j + 1 < F_TILES:
+                gate_branch(j + 1)
+            if j + 3 < F_TILES:
+                copy_weight_tiles(j + 3)
+            if j + 2 < F_TILES:
+                quantise_weight_tile(GATE, j + 2)
+                quantise_weight_tile(UP, j + 2)

@@ -27,10 +27,10 @@ E_BLOCKS = E // P
 RUN = 4
 EPS = 1e-6
 GB_PITCH = 16
-RAW_BUFS = 5
+RAW_BUFS = 8
 GATE = 0
 UP = 1
-GPSIMD_COLS = 256
+GPSIMD_COLS = 384
 FIRST_SHARED_TILE = 3
 
 FLOPS = 2 * TOKENS * E * (E + 2 * F)
@@ -43,50 +43,39 @@ def regroup(copy, grouped, rows):
     )
 
 
+BY_TENSOR, BY_SCALAR, BY_VECTOR = "tensor", "scalar", "vector"
+
+
 def tile_selfdecoderblock_pb_kernel(tc, h_attn, Wo, gamma2, beta2, Wg, Wu, out):
     nc = tc.nc
     h_rows_dram = h_attn.rearrange("b s h d -> b s (h d)")
     wo_dram = Wo.rearrange("h d e -> (h d) e")
-    chunk_order = [(w, c) for c in range(F // CHUNK) for w in (Wg, Wu)]
+    load_order = [(w, c, g) for c in range(F // CHUNK) for w in (GATE, UP) for g in range(PASSES)]
 
     with ExitStack() as ctx:
         ctx.enter_context(tc.manual_schedule())
         keep = ctx.enter_context(tc.tile_pool(name="keep", bufs=1))
         raw_pool = ctx.enter_context(tc.tile_pool(name="raw", bufs=RAW_BUFS))
-        stage = ctx.enter_context(tc.tile_pool(name="stage", bufs=10))
+        stage = ctx.enter_context(tc.tile_pool(name="stage", bufs=9))
         weights = ctx.enter_context(tc.tile_pool(name="weights", bufs=8))
         psum = ctx.enter_context(tc.psum_pool(name="psum", bufs=8))
 
         def bank(shape, dtype):
             return psum.tile(shape, dtype, name="bank")
 
-        def load_wo():
-            raw = raw_pool.tile([P, PASSES, PACK, CHUNK], BF16, name="raw")
-            for g in range(PASSES):
-                nc.sync.dma_start(
-                    out=raw[:, g],
-                    in_=wo_dram[g * K_PASS : (g + 1) * K_PASS, :].rearrange("(p t) n -> p t n", t=PACK),
-                )
-            return raw
+        def load_rows(raw, w, g, first, width):
+            nc.sync.dma_start(
+                out=raw,
+                in_=w[g * K_PASS : (g + 1) * K_PASS, first : first + width].rearrange("(p t) n -> p t n", t=PACK),
+            )
 
-        raws = []
+        raws = {}
 
         def load_chunks(count):
-            for w, c in chunk_order[len(raws) : count]:
-                raw = raw_pool.tile([P, PASSES, PACK, CHUNK], BF16, name="raw")
-                for g in range(PASSES):
-                    nc.sync.dma_start(
-                        out=raw[:, g],
-                        in_=w[g * K_PASS : (g + 1) * K_PASS, c * CHUNK : (c + 1) * CHUNK].rearrange(
-                            "(p t) n -> p t n", t=PACK
-                        ),
-                    )
-                raws.append(raw)
-
-        def copy_unit(copy, raw, g, tile_in_chunk):
-            grouped = stage.tile([P, N_TILE * PACK], BF16, name="grouped", align_bytes=64)
-            regroup(copy, grouped[:], raw[:, g, :, tile_in_chunk * N_TILE : (tile_in_chunk + 1) * N_TILE])
-            return grouped
+            for b, c, g in load_order[len(raws) : count]:
+                raw = raw_pool.tile([P, PACK, CHUNK], BF16, name="raw")
+                load_rows(raw[:], (Wg, Wu)[b], g, c * CHUNK, CHUNK)
+                raws[b, c, g] = raw
 
         def quantise_unit(grouped, operand, g, cols):
             codes, scales = operand
@@ -106,28 +95,60 @@ def tile_selfdecoderblock_pb_kernel(tc, h_attn, Wo, gamma2, beta2, Wg, Wu, out):
         def tokens(m):
             return slice(m * P, (m + 1) * P)
 
+        ident_f32 = keep.tile([P, P], F32, name="ident_f32")
+        make_identity(nc, ident_f32[:])
+        ident_bf16 = keep.tile([P, P], BF16, name="ident_bf16")
+        make_identity(nc, ident_bf16[:])
+
+        def regroup_by_tensor(grouped, rows):
+            width = rows.shape[2]
+            for first in range(0, width, 2 * P):
+                passed = bank([P, 2, P * PACK], BF16)
+                for i in range(2):
+                    start = first + i * P
+                    nc.tensor.matmul(
+                        passed[:, i, :],
+                        lhsT=ident_bf16[:],
+                        rhs=rows[:, :, start : start + P].rearrange("p t c -> p c t"),
+                        start=True,
+                        stop=True,
+                    )
+                nc.scalar.copy(
+                    out=grouped[:, first * PACK : (first + 2 * P) * PACK], in_=passed[:].rearrange("p i x -> p (i x)")
+                )
+
+        def regroup_by(engine, rows):
+            grouped = stage.tile([P, N_TILE * PACK], BF16, name="grouped", align_bytes=64)
+            if engine == BY_TENSOR:
+                regroup_by_tensor(grouped[:], rows)
+            else:
+                regroup(nc.scalar.copy if engine == BY_SCALAR else nc.vector.tensor_copy, grouped[:], rows)
+            return grouped
+
+        shared_tiles = {}
         pieces = {}
         moving = {}
 
-        def copy_weight_piece(copy, grouped, b, j, g, first, width):
-            raw = raws[2 * (j // TILES_PER_CHUNK) + b]
+        def copy_piece(engine, b, j, g, first, width):
             start = (j % TILES_PER_CHUNK) * N_TILE + first
-            regroup(copy, grouped[:], raw[:, g, :, start : start + width])
-            pieces[b, j] = pieces.get((b, j), []) + [(grouped, g, first, width)]
-
-        def copy_weight_unit(b, j, g):
-            copy = nc.scalar.copy if g == 0 else nc.vector.tensor_copy
-            shared = b == UP and g == 1 and j >= FIRST_SHARED_TILE
-            width = N_TILE - GPSIMD_COLS if shared else N_TILE
-            grouped = stage.tile([P, width * PACK], BF16, name="grouped", align_bytes=64)
-            copy_weight_piece(copy, grouped, b, j, g, 0, width)
+            rows = raws[b, j // TILES_PER_CHUNK, g][:, :, start : start + width]
+            if width < N_TILE:
+                if (b, j, g) not in shared_tiles:
+                    shared_tiles[b, j, g] = stage.tile([P, N_TILE * PACK], BF16, name="shared", bufs=1, align_bytes=64)
+                    pieces[b, j] = pieces.get((b, j), []) + [(shared_tiles[b, j, g], g, 0, N_TILE)]
+                copy = {"gpsimd": gpsimd_copy, BY_SCALAR: nc.scalar.copy, BY_VECTOR: nc.vector.tensor_copy}[engine]
+                regroup(copy, shared_tiles[b, j, g][:, first * PACK : (first + width) * PACK], rows)
+            else:
+                pieces[b, j] = pieces.get((b, j), []) + [(regroup_by(engine, rows), g, first, width)]
 
         def gpsimd_copy(out, in_):
             nc.gpsimd.tensor_scalar(out=out, in0=in_, scalar1=1.0, scalar2=0.0, op0=ALU.mult, op1=ALU.add)
 
-        def copy_gpsimd_share(j):
-            grouped = stage.tile([P, GPSIMD_COLS * PACK], BF16, name="grouped_by_gpsimd", bufs=1, align_bytes=64)
-            copy_weight_piece(gpsimd_copy, grouped, UP, j, 1, N_TILE - GPSIMD_COLS, GPSIMD_COLS)
+        def gpsimd_share(b, j, g):
+            copy_piece("gpsimd", b, j, g, N_TILE - GPSIMD_COLS, GPSIMD_COLS)
+
+        def unit(b, j, g, engine, shared=False):
+            copy_piece(engine, b, j, g, 0, N_TILE - GPSIMD_COLS if shared else N_TILE)
 
         def quantise_weight_tile(b, j):
             moving[b, j] = (
@@ -137,8 +158,6 @@ def tile_selfdecoderblock_pb_kernel(tc, h_attn, Wo, gamma2, beta2, Wg, Wu, out):
             for grouped, g, first, width in pieces[b, j]:
                 quantise_unit(grouped, moving[b, j], g, slice(first, first + width))
 
-        ident_f32 = keep.tile([P, P], F32, name="ident_f32")
-        make_identity(nc, ident_f32[:])
         eps = keep.tile([P, 1], F32, name="eps")
         nc.vector.memset(eps[:], EPS)
         warm = keep.tile([P, 2], F32, name="warm")
@@ -148,18 +167,30 @@ def tile_selfdecoderblock_pb_kernel(tc, h_attn, Wo, gamma2, beta2, Wg, Wu, out):
         )
 
         with tc.tile_pool(name="early", bufs=1) as early:
-            wo_raw = load_wo()
+            wo_raw = []
             h_rows = []
-            for m in range(TOK_TILES):
-                rows = early.tile([P, E], BF16, name="h_rows%d" % m)
-                nc.sync.dma_start(out=rows[:], in_=h_rows_dram[m])
-                h_rows.append(rows)
+
+            def load_wo(g):
+                for n in range(TILES_PER_CHUNK):
+                    raw = raw_pool.tile([P, PACK, N_TILE], BF16, name="wo_raw", bufs=PASSES * TILES_PER_CHUNK)
+                    load_rows(raw[:], wo_dram, g, n * N_TILE, N_TILE)
+                    wo_raw.append(raw)
+
+            def load_h():
+                for m in range(TOK_TILES):
+                    rows = early.tile([P, E], BF16, name="h_rows%d" % m)
+                    nc.sync.dma_start(out=rows[:], in_=h_rows_dram[m])
+                    h_rows.append(rows)
+
+            load_h()
+            load_wo(0)
+            load_wo(1)
             gb_rows = early.tile([P, 2, PASSES, GB_PITCH], BF16, name="gb_rows")
             for i, vec in enumerate((gamma2, beta2)):
                 nc.sync.dma_start(
                     out=gb_rows[:, i, :, 0:PACK], in_=vec.rearrange("(g p t) -> p g t", g=PASSES, t=PACK)
                 )
-            load_chunks(RAW_BUFS - 1)
+            load_chunks(RAW_BUFS)
             nc.scalar.activation(out=warm[:, 0:1], in_=eps[:], func=ACT.Sqrt)
 
             wo = (
@@ -167,21 +198,20 @@ def tile_selfdecoderblock_pb_kernel(tc, h_attn, Wo, gamma2, beta2, Wg, Wu, out):
                 early.tile([P, PASSES, E], U8, name="wo_scales", align_bytes=64),
             )
             wo_grouped = {}
-            for g in range(PASSES):
-                wo_grouped[g, 0] = copy_unit(nc.vector.tensor_copy, wo_raw, g, 0)
-                wo_grouped[g, 1] = copy_unit(nc.scalar.copy, wo_raw, g, 1)
-                if g > 0:
-                    quantise_unit(wo_grouped[g - 1, 1], wo, g - 1, slice(N_TILE, 2 * N_TILE))
-                quantise_unit(wo_grouped[g, 0], wo, g, slice(0, N_TILE))
-            quantise_unit(wo_grouped[PASSES - 1, 1], wo, PASSES - 1, slice(N_TILE, 2 * N_TILE))
-            load_chunks(RAW_BUFS)
+
+            def copy_wo(g, n, engine):
+                wo_grouped[g, n] = regroup_by(engine, wo_raw[g * TILES_PER_CHUNK + n][:])
+
+            def quantise_wo(g, n):
+                quantise_unit(wo_grouped[g, n], wo, g, slice(n * N_TILE, (n + 1) * N_TILE))
 
             h = (
                 early.tile([P, PASSES, TOKENS], U32, name="h_codes", align_bytes=64),
                 early.tile([P, PASSES, TOKENS], U8, name="h_scales", align_bytes=64),
             )
             h_grouped = []
-            for m in range(TOK_TILES):
+
+            def turn_h(m):
                 words = bank([P, PASSES * 2, P], F32)
                 for q in range(PASSES * 2):
                     nc.tensor.transpose(
@@ -196,16 +226,21 @@ def tile_selfdecoderblock_pb_kernel(tc, h_attn, Wo, gamma2, beta2, Wg, Wu, out):
                 )
                 h_grouped.append(grouped)
 
-            a = {}
-            for m in range(TOK_TILES):
+            def quantise_h(m):
                 for g in range(PASSES):
                     nc.vector.quantize_mx(
                         out=h[0][:, g, tokens(m)].bitcast(FP8X4), scales=h[1][:, g, tokens(m)], in_=h_grouped[m][:, g, :]
                     )
-                for n in range(TILES_PER_CHUNK):
-                    a[m, n] = bank([P, N_TILE], F32)
-                    for g in range(PASSES):
-                        product(a[m, n][:], h, tokens(m), wo, slice(n * N_TILE, (n + 1) * N_TILE), g)
+
+            a = {}
+
+            def project(q):
+                for g in range(PASSES):
+                    for n in range(TILES_PER_CHUNK):
+                        for m in (2 * q, 2 * q + 1):
+                            if g == 0:
+                                a[m, n] = bank([P, N_TILE], F32)
+                            product(a[m, n][:], h, tokens(m), wo, slice(n * N_TILE, (n + 1) * N_TILE), g)
 
             stats = early.tile([P, TOK_TILES, TILES_PER_CHUNK, 6], F32, name="stats")
             mean_var = early.tile([P, TOK_TILES, 2], F32, name="mean_var")
@@ -213,24 +248,32 @@ def tile_selfdecoderblock_pb_kernel(tc, h_attn, Wo, gamma2, beta2, Wg, Wu, out):
             rstd = early.tile([P, TOK_TILES], F32, name="rstd")
             shift = early.tile([P, TOK_TILES], F32, name="shift")
             normed = [early.tile([P, E], F32, name="normed%d" % m) for m in range(TOK_TILES)]
-
             gain_bias = early.tile([P, 2 * E_BLOCKS], F32, name="gain_bias")
-            nc.vector.tensor_copy(
-                out=gain_bias[:].rearrange("p (i g t) -> p i g t", i=2, t=PACK), in_=gb_rows[:, :, :, 0:PACK]
-            )
-            copy_weight_unit(GATE, 0, 0)
-            copy_weight_unit(GATE, 1, 0)
-            copy_weight_unit(UP, 0, 0)
-            for m in range(TOK_TILES):
-                for n in range(TILES_PER_CHUNK):
-                    nc.vector.bn_stats(out=stats[:, m, n, :], in_=a[m, n][:])
-                nc.vector.bn_aggr(out=mean_var[:, m, :], in_=stats[:, m].rearrange("p n s -> p (n s)"))
-            copy_weight_unit(GATE, 0, 1)
-            nc.scalar.activation(out=std[:], in_=mean_var[:, :, 1], func=ACT.Sqrt, bias=eps[:], scale=1.0)
-            nc.vector.reciprocal(out=rstd[:], in_=std[:])
-            nc.vector.scalar_tensor_tensor(
-                out=shift[:], in0=mean_var[:, :, 0], scalar=-1.0, in1=rstd[:], op0=ALU.mult, op1=ALU.mult
-            )
+            z_planes = early.tile([P, E_BLOCKS, TOKENS], BF16, name="z_planes")
+
+            def load_gain():
+                nc.vector.tensor_copy(
+                    out=gain_bias[:].rearrange("p (i g t) -> p i g t", i=2, t=PACK), in_=gb_rows[:, :, :, 0:PACK]
+                )
+
+            def statistics(q):
+                for m in (2 * q, 2 * q + 1):
+                    for n in range(TILES_PER_CHUNK):
+                        nc.vector.bn_stats(out=stats[:, m, n, :], in_=a[m, n][:])
+                    nc.vector.bn_aggr(out=mean_var[:, m, :], in_=stats[:, m].rearrange("p n s -> p (n s)"))
+
+            def row_scalars(q):
+                pair = slice(2 * q, 2 * q + 2)
+                nc.scalar.activation(out=std[:, pair], in_=mean_var[:, pair, 1], func=ACT.Sqrt, bias=eps[:], scale=1.0)
+                nc.vector.reciprocal(out=rstd[:, pair], in_=std[:, pair])
+                nc.vector.scalar_tensor_tensor(
+                    out=shift[:, pair],
+                    in0=mean_var[:, pair, 0],
+                    scalar=-1.0,
+                    in1=rstd[:, pair],
+                    op0=ALU.mult,
+                    op1=ALU.mult,
+                )
 
             def normalise(m):
                 for n in range(TILES_PER_CHUNK):
@@ -242,12 +285,10 @@ def tile_selfdecoderblock_pb_kernel(tc, h_attn, Wo, gamma2, beta2, Wg, Wu, out):
                         bias=shift[:, m : m + 1],
                     )
 
-            z_planes = early.tile([P, E_BLOCKS, TOKENS], BF16, name="z_planes")
-
             def half_tokens(q):
                 return slice(q * 2 * P, (q + 1) * 2 * P)
 
-            def flip(q):
+            def flip(q, by_vector):
                 for first_block in range(0, E_BLOCKS, 2):
                     flipped = bank([P, 2, 2 * P], F32)
                     for i in range(2):
@@ -262,7 +303,7 @@ def tile_selfdecoderblock_pb_kernel(tc, h_attn, Wo, gamma2, beta2, Wg, Wu, out):
                         r = first_block + i
                         gain = gain_bias[:, r : r + 1]
                         bias = gain_bias[:, E_BLOCKS + r : E_BLOCKS + r + 1]
-                        if q == 0:
+                        if r in by_vector:
                             nc.vector.tensor_scalar(
                                 out=z_planes[:, r, half_tokens(q)],
                                 in0=flipped[:, i, :],
@@ -280,25 +321,60 @@ def tile_selfdecoderblock_pb_kernel(tc, h_attn, Wo, gamma2, beta2, Wg, Wu, out):
                                 bias=bias,
                             )
 
-            copy_weight_unit(GATE, 1, 1)
-            quantise_weight_tile(GATE, 0)
-            quantise_weight_tile(GATE, 1)
-            normalise(0)
-            normalise(1)
-            flip(0)
-            normalise(2)
-            normalise(3)
-            flip(1)
-            nc.scalar.activation(out=warm[:, 1:2], in_=z_planes[:, E_BLOCKS - 1, TOKENS - 1 : TOKENS], func=ACT.Gelu)
-            for q in range(2):
-                z_grouped = []
+            z_grouped = {}
+
+            def regroup_z(q):
                 for g in range(PASSES):
                     grouped = early.tile([P, 2 * P * PACK], BF16, name="z_grouped%d%d" % (q, g), align_bytes=64)
                     regroup(nc.vector.tensor_copy, grouped[:], z_planes[:, g * PACK : (g + 1) * PACK, half_tokens(q)])
-                    z_grouped.append(grouped)
-                copy_weight_unit(UP, q, 1)
+                    z_grouped[q, g] = grouped
+
+            def quantise_z(q):
                 for g in range(PASSES):
-                    quantise_unit(z_grouped[g], z, g, half_tokens(q))
+                    quantise_unit(z_grouped[q, g], z, g, half_tokens(q))
+
+            for m in range(TOK_TILES):
+                turn_h(m)
+                quantise_h(m)
+            copy_wo(0, 0, BY_VECTOR)
+            copy_wo(0, 1, BY_TENSOR)
+            copy_wo(1, 0, BY_VECTOR)
+            quantise_wo(0, 0)
+            copy_wo(1, 1, BY_TENSOR)
+            quantise_wo(0, 1)
+            quantise_wo(1, 0)
+            load_gain()
+            quantise_wo(1, 1)
+            project(0)
+            unit(GATE, 0, 0, BY_TENSOR)
+            project(1)
+            statistics(0)
+            row_scalars(0)
+            statistics(1)
+            normalise(0)
+            normalise(1)
+            row_scalars(1)
+            unit(GATE, 0, 1, BY_VECTOR)
+            flip(0, range(0))
+            normalise(2)
+            normalise(3)
+            unit(UP, 0, 0, BY_TENSOR)
+            flip(1, range(0))
+            unit(UP, 0, 1, BY_VECTOR)
+            quantise_weight_tile(GATE, 0)
+            regroup_z(0)
+            unit(GATE, 1, 0, BY_TENSOR)
+            unit(GATE, 1, 1, BY_TENSOR)
+            quantise_z(0)
+            nc.scalar.activation(out=warm[:, 1:2], in_=z_planes[:, E_BLOCKS - 1, TOKENS - 1 : TOKENS], func=ACT.Gelu)
+            regroup_z(1)
+            quantise_weight_tile(UP, 0)
+            quantise_z(1)
+            unit(UP, 1, 0, BY_TENSOR)
+            unit(UP, 1, 1, BY_TENSOR)
+            load_chunks(RAW_BUFS + 4)
+            quantise_weight_tile(GATE, 1)
+
 
         late = ctx.enter_context(tc.tile_pool(name="late", bufs=1, reuse_waits="tile"))
         gates = {}
@@ -320,27 +396,35 @@ def tile_selfdecoderblock_pb_kernel(tc, h_attn, Wo, gamma2, beta2, Wg, Wu, out):
                 nc.vector.tensor_tensor(out=result[:], in0=gates[j, m][:], in1=acc[:], op=ALU.mult)
                 nc.sync.dma_start(out=out[m, :, j * N_TILE : (j + 1) * N_TILE], in_=result[:])
 
-        def copy_weight_tiles(j):
+        engines = {}
+        for j in range(2, F_TILES):
+            engines[GATE, j, 0] = BY_TENSOR if j < 6 else BY_SCALAR
+            engines[GATE, j, 1] = BY_VECTOR
+            engines[UP, j, 0] = BY_SCALAR
+            engines[UP, j, 1] = BY_VECTOR
+
+        def copy_tile(j):
             for b in (GATE, UP):
                 for g in range(PASSES):
-                    copy_weight_unit(b, j, g)
-            if j % TILES_PER_CHUNK == TILES_PER_CHUNK - 1:
-                load_chunks(RAW_BUFS + j + 1)
+                    if (b, g) != (UP, 1) or j < FIRST_SHARED_TILE:
+                        unit(b, j, g, engines[b, j, g])
+                        if j % TILES_PER_CHUNK == TILES_PER_CHUNK - 1:
+                            load_chunks(RAW_BUFS + 4 * (j // TILES_PER_CHUNK) + 2 * b + g + 1)
 
-        copy_weight_unit(UP, 1, 0)
-        load_chunks(RAW_BUFS + 2)
-        quantise_weight_tile(UP, 0)
         gate_branch(0)
-        copy_weight_tiles(2)
+        copy_tile(2)
         quantise_weight_tile(UP, 1)
         for j in range(F_TILES):
             up_branch(j)
             if FIRST_SHARED_TILE <= j + 2 < F_TILES:
-                copy_gpsimd_share(j + 2)
+                gpsimd_share(UP, j + 2, 1)
+                unit(UP, j + 2, 1, engines[UP, j + 2, 1], True)
+                if j % TILES_PER_CHUNK == TILES_PER_CHUNK - 1:
+                    load_chunks(RAW_BUFS + 4 * ((j + 2) // TILES_PER_CHUNK) + 4)
             if j + 1 < F_TILES:
                 gate_branch(j + 1)
             if j + 3 < F_TILES:
-                copy_weight_tiles(j + 3)
+                copy_tile(j + 3)
             if j + 2 < F_TILES:
                 quantise_weight_tile(GATE, j + 2)
                 quantise_weight_tile(UP, j + 2)

@@ -26,6 +26,7 @@ F_TILES = F // N_TILE
 E_BLOCKS = E // P
 RUN = 4
 EPS = 1e-6
+PSUM_COLS = 256
 GB_PITCH = 16
 RAW_BUFS = 8
 GATE = 0
@@ -101,21 +102,19 @@ def tile_selfdecoderblock_pb_kernel(tc, h_attn, Wo, gamma2, beta2, Wg, Wu, out):
         make_identity(nc, ident_bf16[:])
 
         def regroup_by_tensor(grouped, rows):
-            width = rows.shape[2]
-            for first in range(0, width, 2 * P):
-                passed = bank([P, 2, P * PACK], BF16)
-                for i in range(2):
-                    start = first + i * P
+            for first in range(0, N_TILE, PSUM_COLS):
+                passed = bank([P, PSUM_COLS * PACK], BF16)
+                for start in range(0, PSUM_COLS, P):
                     nc.tensor.matmul(
-                        passed[:, i, :],
+                        passed[:, start * PACK : (start + P) * PACK].rearrange(
+                            "p (c i t) -> p c t i", i=RUN, t=PACK
+                        ),
                         lhsT=ident_bf16[:],
-                        rhs=rows[:, :, start : start + P].rearrange("p t c -> p c t"),
+                        rhs=rows[:, :, first + start : first + start + P].rearrange("p t (c i) -> p c t i", i=RUN),
                         start=True,
                         stop=True,
                     )
-                nc.scalar.copy(
-                    out=grouped[:, first * PACK : (first + 2 * P) * PACK], in_=passed[:].rearrange("p i x -> p (i x)")
-                )
+                nc.scalar.copy(out=grouped[:, first * PACK : (first + PSUM_COLS) * PACK], in_=passed[:])
 
         def regroup_by(engine, rows):
             grouped = stage.tile([P, N_TILE * PACK], BF16, name="grouped", align_bytes=64)
@@ -158,9 +157,9 @@ def tile_selfdecoderblock_pb_kernel(tc, h_attn, Wo, gamma2, beta2, Wg, Wu, out):
             for grouped, g, first, width in pieces[b, j]:
                 quantise_unit(grouped, moving[b, j], g, slice(first, first + width))
 
-        eps = keep.tile([P, 1], F32, name="eps")
-        nc.vector.memset(eps[:], EPS)
-        warm = keep.tile([P, 2], F32, name="warm")
+        zero = keep.tile([P, 1], F32, name="zero")
+        nc.vector.memset(zero[:], 0.0)
+        warm = keep.tile([P, 1], F32, name="warm")
         z = (
             keep.tile([P, PASSES, TOKENS], U32, name="z_codes", align_bytes=64),
             keep.tile([P, PASSES, TOKENS], U8, name="z_scales", align_bytes=64),
@@ -170,11 +169,10 @@ def tile_selfdecoderblock_pb_kernel(tc, h_attn, Wo, gamma2, beta2, Wg, Wu, out):
             wo_raw = []
             h_rows = []
 
-            def load_wo(g):
-                for n in range(TILES_PER_CHUNK):
-                    raw = raw_pool.tile([P, PACK, N_TILE], BF16, name="wo_raw", bufs=PASSES * TILES_PER_CHUNK)
-                    load_rows(raw[:], wo_dram, g, n * N_TILE, N_TILE)
-                    wo_raw.append(raw)
+            def load_wo(g, n):
+                raw = raw_pool.tile([P, PACK, N_TILE], BF16, name="wo_raw", bufs=PASSES * TILES_PER_CHUNK)
+                load_rows(raw[:], wo_dram, g, n * N_TILE, N_TILE)
+                wo_raw.append(raw)
 
             def load_h():
                 for m in range(TOK_TILES):
@@ -182,16 +180,18 @@ def tile_selfdecoderblock_pb_kernel(tc, h_attn, Wo, gamma2, beta2, Wg, Wu, out):
                     nc.sync.dma_start(out=rows[:], in_=h_rows_dram[m])
                     h_rows.append(rows)
 
+            load_wo(0, 0)
             load_h()
-            load_wo(0)
-            load_wo(1)
+            load_wo(0, 1)
+            load_wo(1, 0)
+            load_wo(1, 1)
             gb_rows = early.tile([P, 2, PASSES, GB_PITCH], BF16, name="gb_rows")
             for i, vec in enumerate((gamma2, beta2)):
                 nc.sync.dma_start(
                     out=gb_rows[:, i, :, 0:PACK], in_=vec.rearrange("(g p t) -> p g t", g=PASSES, t=PACK)
                 )
             load_chunks(RAW_BUFS)
-            nc.scalar.activation(out=warm[:, 0:1], in_=eps[:], func=ACT.Sqrt)
+            nc.scalar.activation(out=warm[:, 0:1], in_=zero[:], func=ACT.Gelu)
 
             wo = (
                 early.tile([P, PASSES, E], U32, name="wo_codes", align_bytes=64),
@@ -244,7 +244,9 @@ def tile_selfdecoderblock_pb_kernel(tc, h_attn, Wo, gamma2, beta2, Wg, Wu, out):
 
             stats = early.tile([P, TOK_TILES, TILES_PER_CHUNK, 6], F32, name="stats")
             mean_var = early.tile([P, TOK_TILES, 2], F32, name="mean_var")
-            std = early.tile([P, TOK_TILES], F32, name="std")
+            spread = early.tile([P, TOK_TILES], F32, name="spread")
+            minus_half = early.tile([P, TOK_TILES], F32, name="minus_half")
+            nc.gpsimd.memset(minus_half[:], -0.5)
             rstd = early.tile([P, TOK_TILES], F32, name="rstd")
             shift = early.tile([P, TOK_TILES], F32, name="shift")
             normed = [early.tile([P, E], F32, name="normed%d" % m) for m in range(TOK_TILES)]
@@ -264,8 +266,10 @@ def tile_selfdecoderblock_pb_kernel(tc, h_attn, Wo, gamma2, beta2, Wg, Wu, out):
 
             def row_scalars(q):
                 pair = slice(2 * q, 2 * q + 2)
-                nc.scalar.activation(out=std[:, pair], in_=mean_var[:, pair, 1], func=ACT.Sqrt, bias=eps[:], scale=1.0)
-                nc.vector.reciprocal(out=rstd[:, pair], in_=std[:, pair])
+                nc.gpsimd.tensor_scalar(
+                    out=spread[:, pair], in0=mean_var[:, pair, 1], scalar1=1.0, scalar2=EPS, op0=ALU.mult, op1=ALU.add
+                )
+                nc.gpsimd.tensor_tensor(out=rstd[:, pair], in0=spread[:, pair], in1=minus_half[:, pair], op=ALU.pow)
                 nc.vector.scalar_tensor_tensor(
                     out=shift[:, pair],
                     in0=mean_var[:, pair, 0],
@@ -333,47 +337,46 @@ def tile_selfdecoderblock_pb_kernel(tc, h_attn, Wo, gamma2, beta2, Wg, Wu, out):
                 for g in range(PASSES):
                     quantise_unit(z_grouped[q, g], z, g, half_tokens(q))
 
+            copy_wo(0, 0, BY_VECTOR)
             for m in range(TOK_TILES):
                 turn_h(m)
                 quantise_h(m)
-            copy_wo(0, 0, BY_VECTOR)
-            copy_wo(0, 1, BY_TENSOR)
-            copy_wo(1, 0, BY_VECTOR)
             quantise_wo(0, 0)
-            copy_wo(1, 1, BY_TENSOR)
+            copy_wo(0, 1, BY_SCALAR)
+            copy_wo(1, 0, BY_VECTOR)
+            copy_wo(1, 1, BY_VECTOR)
             quantise_wo(0, 1)
             quantise_wo(1, 0)
-            load_gain()
             quantise_wo(1, 1)
+            load_gain()
             project(0)
-            unit(GATE, 0, 0, BY_TENSOR)
+            unit(GATE, 0, 0, BY_SCALAR)
             project(1)
             statistics(0)
             row_scalars(0)
-            statistics(1)
+            unit(GATE, 0, 1, BY_VECTOR)
             normalise(0)
             normalise(1)
+            unit(GATE, 1, 0, BY_TENSOR)
+            statistics(1)
             row_scalars(1)
-            unit(GATE, 0, 1, BY_VECTOR)
             flip(0, range(0))
+            unit(UP, 0, 0, BY_TENSOR)
+            unit(GATE, 1, 1, BY_VECTOR)
             normalise(2)
             normalise(3)
-            unit(UP, 0, 0, BY_TENSOR)
-            flip(1, range(0))
-            unit(UP, 0, 1, BY_VECTOR)
             quantise_weight_tile(GATE, 0)
             regroup_z(0)
-            unit(GATE, 1, 0, BY_TENSOR)
-            unit(GATE, 1, 1, BY_TENSOR)
+            flip(1, range(0))
+            unit(UP, 0, 1, BY_VECTOR)
             quantise_z(0)
-            nc.scalar.activation(out=warm[:, 1:2], in_=z_planes[:, E_BLOCKS - 1, TOKENS - 1 : TOKENS], func=ACT.Gelu)
-            regroup_z(1)
-            quantise_weight_tile(UP, 0)
-            quantise_z(1)
             unit(UP, 1, 0, BY_TENSOR)
             unit(UP, 1, 1, BY_TENSOR)
             load_chunks(RAW_BUFS + 4)
+            quantise_weight_tile(UP, 0)
+            regroup_z(1)
             quantise_weight_tile(GATE, 1)
+            quantise_z(1)
 
 
         late = ctx.enter_context(tc.tile_pool(name="late", bufs=1, reuse_waits="tile"))

@@ -32,7 +32,7 @@ RAW_BUFS = 8
 GATE = 0
 UP = 1
 GPSIMD_COLS = 384
-FIRST_SHARED_TILE = 3
+FIRST_SHARED_TILE = 8
 
 FLOPS = 2 * TOKENS * E * (E + 2 * F)
 
@@ -120,8 +120,12 @@ def tile_selfdecoderblock_pb_kernel(tc, h_attn, Wo, gamma2, beta2, Wg, Wu, out):
             grouped = stage.tile([P, N_TILE * PACK], BF16, name="grouped", align_bytes=64)
             if engine == BY_TENSOR:
                 regroup_by_tensor(grouped[:], rows)
-            else:
+            elif engine in (BY_SCALAR, BY_VECTOR):
                 regroup(nc.scalar.copy if engine == BY_SCALAR else nc.vector.tensor_copy, grouped[:], rows)
+            else:
+                cut = N_TILE - engine
+                regroup(nc.scalar.copy, grouped[:, 0 : cut * PACK], rows[:, :, 0:cut])
+                regroup(nc.vector.tensor_copy, grouped[:, cut * PACK :], rows[:, :, cut:])
             return grouped
 
         shared_tiles = {}
@@ -344,38 +348,38 @@ def tile_selfdecoderblock_pb_kernel(tc, h_attn, Wo, gamma2, beta2, Wg, Wu, out):
             quantise_wo(0, 0)
             copy_wo(0, 1, BY_SCALAR)
             copy_wo(1, 0, BY_VECTOR)
-            copy_wo(1, 1, BY_VECTOR)
+            copy_wo(1, 1, N_TILE // 2)
             quantise_wo(0, 1)
             quantise_wo(1, 0)
             quantise_wo(1, 1)
             load_gain()
             project(0)
-            unit(GATE, 0, 0, BY_SCALAR)
             project(1)
+            unit(GATE, 0, 0, BY_SCALAR)
             statistics(0)
             row_scalars(0)
-            unit(GATE, 0, 1, BY_VECTOR)
+            statistics(1)
+            unit(GATE, 1, 0, BY_SCALAR)
             normalise(0)
             normalise(1)
-            unit(GATE, 1, 0, BY_TENSOR)
-            statistics(1)
+            unit(GATE, 0, 1, BY_VECTOR)
             row_scalars(1)
+            quantise_weight_tile(GATE, 0)
             flip(0, range(0))
-            unit(UP, 0, 0, BY_TENSOR)
+            unit(UP, 0, 0, BY_SCALAR)
             unit(GATE, 1, 1, BY_VECTOR)
+            unit(UP, 0, 1, BY_VECTOR)
             normalise(2)
             normalise(3)
-            quantise_weight_tile(GATE, 0)
-            regroup_z(0)
             flip(1, range(0))
-            unit(UP, 0, 1, BY_VECTOR)
+            regroup_z(0)
+            quantise_weight_tile(GATE, 1)
             quantise_z(0)
-            unit(UP, 1, 0, BY_TENSOR)
-            unit(UP, 1, 1, BY_TENSOR)
-            load_chunks(RAW_BUFS + 4)
+            unit(UP, 1, 0, BY_SCALAR)
             quantise_weight_tile(UP, 0)
             regroup_z(1)
-            quantise_weight_tile(GATE, 1)
+            unit(UP, 1, 1, BY_VECTOR)
+            load_chunks(RAW_BUFS + 4)
             quantise_z(1)
 
 
@@ -401,7 +405,7 @@ def tile_selfdecoderblock_pb_kernel(tc, h_attn, Wo, gamma2, beta2, Wg, Wu, out):
 
         engines = {}
         for j in range(2, F_TILES):
-            engines[GATE, j, 0] = BY_TENSOR if j < 6 else BY_SCALAR
+            engines[GATE, j, 0] = BY_SCALAR
             engines[GATE, j, 1] = BY_VECTOR
             engines[UP, j, 0] = BY_SCALAR
             engines[UP, j, 1] = BY_VECTOR

@@ -32,7 +32,7 @@ RAW_BUFS = 8
 GATE = 0
 UP = 1
 GPSIMD_COLS = 384
-FIRST_SHARED_TILE = 8
+FIRST_SHARED_TILE = 2
 
 FLOPS = 2 * TOKENS * E * (E + 2 * F)
 
@@ -139,8 +139,11 @@ def tile_selfdecoderblock_pb_kernel(tc, h_attn, Wo, gamma2, beta2, Wg, Wu, out):
                 if (b, j, g) not in shared_tiles:
                     shared_tiles[b, j, g] = stage.tile([P, N_TILE * PACK], BF16, name="shared", bufs=1, align_bytes=64)
                     pieces[b, j] = pieces.get((b, j), []) + [(shared_tiles[b, j, g], g, 0, N_TILE)]
-                copy = {"gpsimd": gpsimd_copy, BY_SCALAR: nc.scalar.copy, BY_VECTOR: nc.vector.tensor_copy}[engine]
-                regroup(copy, shared_tiles[b, j, g][:, first * PACK : (first + width) * PACK], rows)
+                part = shared_tiles[b, j, g][:, first * PACK : (first + width) * PACK]
+                if engine == "gpsimd":
+                    gpsimd_copy(out=part.rearrange("p (c t) -> p c t", t=PACK), in_=rows.rearrange("p t c -> p c t"))
+                else:
+                    regroup({BY_SCALAR: nc.scalar.copy, BY_VECTOR: nc.vector.tensor_copy}[engine], part, rows)
             else:
                 pieces[b, j] = pieces.get((b, j), []) + [(regroup_by(engine, rows), g, first, width)]
 
@@ -274,6 +277,9 @@ def tile_selfdecoderblock_pb_kernel(tc, h_attn, Wo, gamma2, beta2, Wg, Wu, out):
                     out=spread[:, pair], in0=mean_var[:, pair, 1], scalar1=1.0, scalar2=EPS, op0=ALU.mult, op1=ALU.add
                 )
                 nc.gpsimd.tensor_tensor(out=rstd[:, pair], in0=spread[:, pair], in1=minus_half[:, pair], op=ALU.pow)
+
+            def row_shift(q):
+                pair = slice(2 * q, 2 * q + 2)
                 nc.vector.scalar_tensor_tensor(
                     out=shift[:, pair],
                     in0=mean_var[:, pair, 0],
@@ -341,7 +347,7 @@ def tile_selfdecoderblock_pb_kernel(tc, h_attn, Wo, gamma2, beta2, Wg, Wu, out):
                 for g in range(PASSES):
                     quantise_unit(z_grouped[q, g], z, g, half_tokens(q))
 
-            copy_wo(0, 0, BY_VECTOR)
+            copy_wo(0, 0, N_TILE // 2)
             for m in range(TOK_TILES):
                 turn_h(m)
                 quantise_h(m)
@@ -358,12 +364,15 @@ def tile_selfdecoderblock_pb_kernel(tc, h_attn, Wo, gamma2, beta2, Wg, Wu, out):
             unit(GATE, 0, 0, BY_SCALAR)
             statistics(0)
             row_scalars(0)
+            gpsimd_share(GATE, 0, 1)
             statistics(1)
+            row_shift(0)
             unit(GATE, 1, 0, BY_SCALAR)
             normalise(0)
             normalise(1)
-            unit(GATE, 0, 1, BY_VECTOR)
             row_scalars(1)
+            unit(GATE, 0, 1, BY_VECTOR, True)
+            row_shift(1)
             quantise_weight_tile(GATE, 0)
             flip(0, range(0))
             unit(UP, 0, 0, BY_SCALAR)

@@ -16,49 +16,49 @@ PACK = 4
 K_PASS = P * PACK
 TOKENS = 512
 TOK_TILES = TOKENS // P
+HALVES = 2
+HALF = TOKENS // HALVES
 E = 1024
 F = 4096
 PASSES = E // K_PASS
 N_TILE = 512
+UNIT = N_TILE * PACK
 CHUNK = 1024
 TILES_PER_CHUNK = CHUNK // N_TILE
 F_TILES = F // N_TILE
 E_BLOCKS = E // P
-RUN = 4
+RUN_V = 4
+RUN_S = 4
 EPS = 1e-6
-PSUM_COLS = 256
 GB_PITCH = 16
 RAW_BUFS = 8
 GATE = 0
 UP = 1
 GPSIMD_COLS = 384
-FIRST_SHARED_TILE = 2
+VECTOR_COLS = 64
 
 FLOPS = 2 * TOKENS * E * (E + 2 * F)
 
 
-def regroup(copy, grouped, rows):
+def regroup(copy, grouped, rows, run):
     copy(
-        out=grouped.rearrange("p (c i t) -> p c t i", i=RUN, t=PACK),
-        in_=rows.rearrange("p t (c i) -> p c t i", i=RUN),
+        out=grouped.rearrange("p (c i t) -> p c t i", i=run, t=PACK),
+        in_=rows.rearrange("p t (c i) -> p c t i", i=run),
     )
-
-
-BY_TENSOR, BY_SCALAR, BY_VECTOR = "tensor", "scalar", "vector"
 
 
 def tile_selfdecoderblock_pb_kernel(tc, h_attn, Wo, gamma2, beta2, Wg, Wu, out):
     nc = tc.nc
     h_rows_dram = h_attn.rearrange("b s h d -> b s (h d)")
     wo_dram = Wo.rearrange("h d e -> (h d) e")
-    load_order = [(w, c, g) for c in range(F // CHUNK) for w in (GATE, UP) for g in range(PASSES)]
+    load_order = [(b, c, g) for c in range(F // CHUNK) for b in (GATE, UP) for g in range(PASSES)]
 
     with ExitStack() as ctx:
         ctx.enter_context(tc.manual_schedule())
         keep = ctx.enter_context(tc.tile_pool(name="keep", bufs=1))
         raw_pool = ctx.enter_context(tc.tile_pool(name="raw", bufs=RAW_BUFS))
-        stage = ctx.enter_context(tc.tile_pool(name="stage", bufs=9))
-        weights = ctx.enter_context(tc.tile_pool(name="weights", bufs=8))
+        stage = ctx.enter_context(tc.tile_pool(name="stage", bufs=1))
+        weights = ctx.enter_context(tc.tile_pool(name="weights", bufs=6))
         psum = ctx.enter_context(tc.psum_pool(name="psum", bufs=8))
 
         def bank(shape, dtype):
@@ -78,108 +78,103 @@ def tile_selfdecoderblock_pb_kernel(tc, h_attn, Wo, gamma2, beta2, Wg, Wu, out):
                 load_rows(raw[:], (Wg, Wu)[b], g, c * CHUNK, CHUNK)
                 raws[b, c, g] = raw
 
-        def quantise_unit(grouped, operand, g, cols):
-            codes, scales = operand
-            nc.vector.quantize_mx(out=codes[:, g, cols].bitcast(FP8X4), scales=scales[:, g, cols], in_=grouped[:])
-
-        def product(acc, left, left_cols, right, right_cols, g):
+        def product(acc, left, right, g):
             nc.tensor.matmul_mx(
                 out=acc,
-                lhsT=left[0][:, g, left_cols].bitcast(FP8X4),
-                lhsT_scale=left[1][:, g, left_cols],
-                rhs=right[0][:, g, right_cols].bitcast(FP8X4),
-                rhs_scale=right[1][:, g, right_cols],
+                lhsT=left[0].bitcast(FP8X4),
+                lhsT_scale=left[1],
+                rhs=right[0].bitcast(FP8X4),
+                rhs_scale=right[1],
                 start=(g == 0),
                 stop=(g == PASSES - 1),
             )
 
-        def tokens(m):
-            return slice(m * P, (m + 1) * P)
+        def by_scalar(grouped, rows):
+            regroup(nc.scalar.copy, grouped, rows, RUN_S)
+
+        def by_vector(grouped, rows):
+            regroup(nc.vector.tensor_copy, grouped, rows, RUN_V)
+
+        def by_both(cols):
+            def copy(grouped, rows):
+                cut = N_TILE - cols
+                by_scalar(grouped[:, 0 : cut * PACK], rows[:, :, 0:cut])
+                by_vector(grouped[:, cut * PACK :], rows[:, :, cut:])
+
+            return copy
+
+        def by_gpsimd(grouped, rows):
+            nc.gpsimd.tensor_scalar(
+                out=grouped.rearrange("p (c t) -> p c t", t=PACK),
+                in0=rows.rearrange("p t c -> p c t"),
+                scalar1=1.0,
+                scalar2=0.0,
+                op0=ALU.mult,
+                op1=ALU.add,
+            )
+
+        grouped_units = {}
+        moving = {}
+
+        def raw_unit(b, j, g):
+            start = (j % TILES_PER_CHUNK) * N_TILE
+            return raws[b, j // TILES_PER_CHUNK, g][:, :, start : start + N_TILE]
+
+        def unit(copy, b, j, g):
+            if b == UP:
+                if g == 0:
+                    grouped_units[b, j] = stage.tile(
+                        [P, PASSES, UNIT], BF16, name="pair", bufs=3, align_bytes=64
+                    )
+                grouped = grouped_units[b, j][:, g, :]
+            else:
+                tile = stage.tile([P, UNIT], BF16, name="single", bufs=6, align_bytes=64)
+                grouped_units[b, j, g] = tile
+                grouped = tile[:]
+            copy(grouped, raw_unit(b, j, g))
+
+        def shared_unit_by_gpsimd(j):
+            tile = stage.tile([P, UNIT], BF16, name="shared", bufs=1, align_bytes=64)
+            grouped_units[GATE, j, 1] = tile
+            cut = N_TILE - GPSIMD_COLS
+            by_gpsimd(tile[:, cut * PACK :], raw_unit(GATE, j, 1)[:, :, cut:])
+
+        def shared_unit_by_vector(j):
+            cut = N_TILE - GPSIMD_COLS
+            by_vector(grouped_units[GATE, j, 1][:, 0 : cut * PACK], raw_unit(GATE, j, 1)[:, :, 0:cut])
+
+        def quantise_tile(b, j):
+            codes = weights.tile([P, PASSES, N_TILE], U32, name="codes", align_bytes=64)
+            scales = weights.tile([P, PASSES, N_TILE], U8, name="scales", align_bytes=64)
+            if b == UP:
+                nc.vector.quantize_mx(
+                    out=codes[:].rearrange("p g n -> p (g n)").bitcast(FP8X4),
+                    scales=scales[:].rearrange("p g n -> p (g n)"),
+                    in_=grouped_units[b, j][:].rearrange("p g x -> p (g x)"),
+                )
+            else:
+                for g in range(PASSES):
+                    nc.vector.quantize_mx(
+                        out=codes[:, g, :].bitcast(FP8X4), scales=scales[:, g, :], in_=grouped_units[b, j, g][:]
+                    )
+            moving[b, j] = (codes, scales)
 
         ident_f32 = keep.tile([P, P], F32, name="ident_f32")
         make_identity(nc, ident_f32[:])
-        ident_bf16 = keep.tile([P, P], BF16, name="ident_bf16")
-        make_identity(nc, ident_bf16[:])
-
-        def regroup_by_tensor(grouped, rows):
-            for first in range(0, N_TILE, PSUM_COLS):
-                passed = bank([P, PSUM_COLS * PACK], BF16)
-                for start in range(0, PSUM_COLS, P):
-                    nc.tensor.matmul(
-                        passed[:, start * PACK : (start + P) * PACK].rearrange(
-                            "p (c i t) -> p c t i", i=RUN, t=PACK
-                        ),
-                        lhsT=ident_bf16[:],
-                        rhs=rows[:, :, first + start : first + start + P].rearrange("p t (c i) -> p c t i", i=RUN),
-                        start=True,
-                        stop=True,
-                    )
-                nc.scalar.copy(out=grouped[:, first * PACK : (first + PSUM_COLS) * PACK], in_=passed[:])
-
-        def regroup_by(engine, rows):
-            grouped = stage.tile([P, N_TILE * PACK], BF16, name="grouped", align_bytes=64)
-            if engine == BY_TENSOR:
-                regroup_by_tensor(grouped[:], rows)
-            elif engine in (BY_SCALAR, BY_VECTOR):
-                regroup(nc.scalar.copy if engine == BY_SCALAR else nc.vector.tensor_copy, grouped[:], rows)
-            else:
-                cut = N_TILE - engine
-                regroup(nc.scalar.copy, grouped[:, 0 : cut * PACK], rows[:, :, 0:cut])
-                regroup(nc.vector.tensor_copy, grouped[:, cut * PACK :], rows[:, :, cut:])
-            return grouped
-
-        shared_tiles = {}
-        pieces = {}
-        moving = {}
-
-        def copy_piece(engine, b, j, g, first, width):
-            start = (j % TILES_PER_CHUNK) * N_TILE + first
-            rows = raws[b, j // TILES_PER_CHUNK, g][:, :, start : start + width]
-            if width < N_TILE:
-                if (b, j, g) not in shared_tiles:
-                    shared_tiles[b, j, g] = stage.tile([P, N_TILE * PACK], BF16, name="shared", bufs=1, align_bytes=64)
-                    pieces[b, j] = pieces.get((b, j), []) + [(shared_tiles[b, j, g], g, 0, N_TILE)]
-                part = shared_tiles[b, j, g][:, first * PACK : (first + width) * PACK]
-                if engine == "gpsimd":
-                    gpsimd_copy(out=part.rearrange("p (c t) -> p c t", t=PACK), in_=rows.rearrange("p t c -> p c t"))
-                else:
-                    regroup({BY_SCALAR: nc.scalar.copy, BY_VECTOR: nc.vector.tensor_copy}[engine], part, rows)
-            else:
-                pieces[b, j] = pieces.get((b, j), []) + [(regroup_by(engine, rows), g, first, width)]
-
-        def gpsimd_copy(out, in_):
-            nc.gpsimd.tensor_scalar(out=out, in0=in_, scalar1=1.0, scalar2=0.0, op0=ALU.mult, op1=ALU.add)
-
-        def gpsimd_share(b, j, g):
-            copy_piece("gpsimd", b, j, g, N_TILE - GPSIMD_COLS, GPSIMD_COLS)
-
-        def unit(b, j, g, engine, shared=False):
-            copy_piece(engine, b, j, g, 0, N_TILE - GPSIMD_COLS if shared else N_TILE)
-
-        def quantise_weight_tile(b, j):
-            moving[b, j] = (
-                weights.tile([P, PASSES, N_TILE], U32, name="codes", align_bytes=64),
-                weights.tile([P, PASSES, N_TILE], U8, name="scales", align_bytes=64),
-            )
-            for grouped, g, first, width in pieces[b, j]:
-                quantise_unit(grouped, moving[b, j], g, slice(first, first + width))
-
         zero = keep.tile([P, 1], F32, name="zero")
         nc.vector.memset(zero[:], 0.0)
         warm = keep.tile([P, 1], F32, name="warm")
-        z = (
-            keep.tile([P, PASSES, TOKENS], U32, name="z_codes", align_bytes=64),
-            keep.tile([P, PASSES, TOKENS], U8, name="z_scales", align_bytes=64),
-        )
+        z_codes = keep.tile([P, HALVES, PASSES, HALF], U32, name="z_codes", align_bytes=64)
+        z_scales = keep.tile([P, HALVES, PASSES, HALF], U8, name="z_scales", align_bytes=64)
 
         with tc.tile_pool(name="early", bufs=1) as early:
-            wo_raw = []
+            wo_raw = {}
             h_rows = []
 
             def load_wo(g, n):
-                raw = raw_pool.tile([P, PACK, N_TILE], BF16, name="wo_raw", bufs=PASSES * TILES_PER_CHUNK)
+                raw = early.tile([P, PACK, N_TILE], BF16, name="wide", bufs=4)
                 load_rows(raw[:], wo_dram, g, n * N_TILE, N_TILE)
-                wo_raw.append(raw)
+                wo_raw[g, n] = raw
 
             def load_h():
                 for m in range(TOK_TILES):
@@ -198,33 +193,33 @@ def tile_selfdecoderblock_pb_kernel(tc, h_attn, Wo, gamma2, beta2, Wg, Wu, out):
                     out=gb_rows[:, i, :, 0:PACK], in_=vec.rearrange("(g p t) -> p g t", g=PASSES, t=PACK)
                 )
             load_chunks(RAW_BUFS)
-            nc.scalar.activation(out=warm[:, 0:1], in_=zero[:], func=ACT.Gelu)
+            nc.scalar.activation(out=warm[:], in_=zero[:], func=ACT.Gelu)
 
-            wo = (
-                early.tile([P, PASSES, E], U32, name="wo_codes", align_bytes=64),
-                early.tile([P, PASSES, E], U8, name="wo_scales", align_bytes=64),
-            )
+            wo_codes = early.tile([P, PASSES, E], U32, name="wo_codes", align_bytes=64)
+            wo_scales = early.tile([P, PASSES, E], U8, name="wo_scales", align_bytes=64)
             wo_grouped = {}
 
-            def copy_wo(g, n, engine):
-                wo_grouped[g, n] = regroup_by(engine, wo_raw[g * TILES_PER_CHUNK + n][:])
+            def copy_wo(copy, g, n):
+                grouped = stage.tile([P, UNIT], BF16, name="single", bufs=6, align_bytes=64)
+                copy(grouped[:], wo_raw[g, n][:])
+                wo_grouped[g, n] = grouped
 
             def quantise_wo(g, n):
-                quantise_unit(wo_grouped[g, n], wo, g, slice(n * N_TILE, (n + 1) * N_TILE))
+                cols = slice(n * N_TILE, (n + 1) * N_TILE)
+                nc.vector.quantize_mx(
+                    out=wo_codes[:, g, cols].bitcast(FP8X4), scales=wo_scales[:, g, cols], in_=wo_grouped[g, n][:]
+                )
 
-            h = (
-                early.tile([P, PASSES, TOKENS], U32, name="h_codes", align_bytes=64),
-                early.tile([P, PASSES, TOKENS], U8, name="h_scales", align_bytes=64),
-            )
+            h_codes = early.tile([P, TOK_TILES, PASSES, P], U32, name="h_codes", align_bytes=64)
+            h_scales = early.tile([P, TOK_TILES, PASSES, P], U8, name="h_scales", align_bytes=64)
             h_grouped = []
 
             def turn_h(m):
                 words = bank([P, PASSES * 2, P], F32)
                 for q in range(PASSES * 2):
+                    first = (q // 2) * 2 * P + q % 2
                     nc.tensor.transpose(
-                        words[:, q, :],
-                        h_rows[m][:].bitcast(F32)[:, (q // 2) * 2 * P + q % 2 : (q // 2 + 1) * 2 * P : 2],
-                        ident_f32[:],
+                        words[:, q, :], h_rows[m][:].bitcast(F32)[:, first : (q // 2 + 1) * 2 * P : 2], ident_f32[:]
                     )
                 grouped = early.tile([P, PASSES, P * PACK], BF16, name="h_grouped%d" % m, align_bytes=64)
                 nc.scalar.copy(
@@ -234,20 +229,27 @@ def tile_selfdecoderblock_pb_kernel(tc, h_attn, Wo, gamma2, beta2, Wg, Wu, out):
                 h_grouped.append(grouped)
 
             def quantise_h(m):
-                for g in range(PASSES):
-                    nc.vector.quantize_mx(
-                        out=h[0][:, g, tokens(m)].bitcast(FP8X4), scales=h[1][:, g, tokens(m)], in_=h_grouped[m][:, g, :]
-                    )
+                nc.vector.quantize_mx(
+                    out=h_codes[:, m].rearrange("p g n -> p (g n)").bitcast(FP8X4),
+                    scales=h_scales[:, m].rearrange("p g n -> p (g n)"),
+                    in_=h_grouped[m][:].rearrange("p g x -> p (g x)"),
+                )
 
             a = {}
 
             def project(q):
                 for g in range(PASSES):
                     for n in range(TILES_PER_CHUNK):
+                        cols = slice(n * N_TILE, (n + 1) * N_TILE)
                         for m in (2 * q, 2 * q + 1):
                             if g == 0:
                                 a[m, n] = bank([P, N_TILE], F32)
-                            product(a[m, n][:], h, tokens(m), wo, slice(n * N_TILE, (n + 1) * N_TILE), g)
+                            product(
+                                a[m, n][:],
+                                (h_codes[:, m, g, :], h_scales[:, m, g, :]),
+                                (wo_codes[:, g, cols], wo_scales[:, g, cols]),
+                                g,
+                            )
 
             stats = early.tile([P, TOK_TILES, TILES_PER_CHUNK, 6], F32, name="stats")
             mean_var = early.tile([P, TOK_TILES, 2], F32, name="mean_var")
@@ -256,29 +258,29 @@ def tile_selfdecoderblock_pb_kernel(tc, h_attn, Wo, gamma2, beta2, Wg, Wu, out):
             nc.gpsimd.memset(minus_half[:], -0.5)
             rstd = early.tile([P, TOK_TILES], F32, name="rstd")
             shift = early.tile([P, TOK_TILES], F32, name="shift")
-            normed = [early.tile([P, E], F32, name="normed%d" % m) for m in range(TOK_TILES)]
+            normed = {}
             gain_bias = early.tile([P, 2 * E_BLOCKS], F32, name="gain_bias")
             z_planes = early.tile([P, E_BLOCKS, TOKENS], BF16, name="z_planes")
+            z_grouped = early.tile([P, HALVES, PASSES, HALF * PACK], BF16, name="z_grouped", align_bytes=64)
 
             def load_gain():
                 nc.vector.tensor_copy(
                     out=gain_bias[:].rearrange("p (i g t) -> p i g t", i=2, t=PACK), in_=gb_rows[:, :, :, 0:PACK]
                 )
 
-            def statistics(q):
-                for m in (2 * q, 2 * q + 1):
-                    for n in range(TILES_PER_CHUNK):
-                        nc.vector.bn_stats(out=stats[:, m, n, :], in_=a[m, n][:])
-                    nc.vector.bn_aggr(out=mean_var[:, m, :], in_=stats[:, m].rearrange("p n s -> p (n s)"))
+            def statistics(m):
+                for n in range(TILES_PER_CHUNK):
+                    nc.vector.bn_stats(out=stats[:, m, n, :], in_=a[m, n][:])
+                nc.vector.bn_aggr(out=mean_var[:, m, :], in_=stats[:, m].rearrange("p n s -> p (n s)"))
 
-            def row_scalars(q):
+            def row_scales(q):
                 pair = slice(2 * q, 2 * q + 2)
                 nc.gpsimd.tensor_scalar(
                     out=spread[:, pair], in0=mean_var[:, pair, 1], scalar1=1.0, scalar2=EPS, op0=ALU.mult, op1=ALU.add
                 )
                 nc.gpsimd.tensor_tensor(out=rstd[:, pair], in0=spread[:, pair], in1=minus_half[:, pair], op=ALU.pow)
 
-            def row_shift(q):
+            def row_shifts(q):
                 pair = slice(2 * q, 2 * q + 2)
                 nc.vector.scalar_tensor_tensor(
                     out=shift[:, pair],
@@ -290,6 +292,7 @@ def tile_selfdecoderblock_pb_kernel(tc, h_attn, Wo, gamma2, beta2, Wg, Wu, out):
                 )
 
             def normalise(m):
+                normed[m] = early.tile([P, E], F32, name="wide", bufs=4)
                 for n in range(TILES_PER_CHUNK):
                     nc.scalar.activation(
                         out=normed[m][:, n * N_TILE : (n + 1) * N_TILE].rearrange("p (t q) -> p t q", t=PACK),
@@ -299,27 +302,27 @@ def tile_selfdecoderblock_pb_kernel(tc, h_attn, Wo, gamma2, beta2, Wg, Wu, out):
                         bias=shift[:, m : m + 1],
                     )
 
-            def half_tokens(q):
-                return slice(q * 2 * P, (q + 1) * 2 * P)
+            def half(q):
+                return slice(q * HALF, (q + 1) * HALF)
 
-            def flip(q, by_vector):
+            def flip(q, vector_blocks):
                 for first_block in range(0, E_BLOCKS, 2):
-                    flipped = bank([P, 2, 2 * P], F32)
+                    flipped = bank([P, 2, HALF], F32)
                     for i in range(2):
                         r = first_block + i
-                        for tile_in_half in range(2):
+                        for s in range(2):
                             nc.tensor.transpose(
-                                flipped[:, i, tokens(tile_in_half)],
-                                normed[2 * q + tile_in_half][:, r * P : (r + 1) * P],
+                                flipped[:, i, s * P : (s + 1) * P],
+                                normed[2 * q + s][:, r * P : (r + 1) * P],
                                 ident_f32[:],
                             )
                     for i in range(2):
                         r = first_block + i
                         gain = gain_bias[:, r : r + 1]
                         bias = gain_bias[:, E_BLOCKS + r : E_BLOCKS + r + 1]
-                        if r in by_vector:
+                        if r in vector_blocks:
                             nc.vector.tensor_scalar(
-                                out=z_planes[:, r, half_tokens(q)],
+                                out=z_planes[:, r, half(q)],
                                 in0=flipped[:, i, :],
                                 scalar1=gain,
                                 scalar2=bias,
@@ -328,119 +331,117 @@ def tile_selfdecoderblock_pb_kernel(tc, h_attn, Wo, gamma2, beta2, Wg, Wu, out):
                             )
                         else:
                             nc.scalar.activation(
-                                out=z_planes[:, r, half_tokens(q)],
+                                out=z_planes[:, r, half(q)],
                                 in_=flipped[:, i, :],
                                 func=ACT.Identity,
                                 scale=gain,
                                 bias=bias,
                             )
 
-            z_grouped = {}
-
-            def regroup_z(q):
-                for g in range(PASSES):
-                    grouped = early.tile([P, 2 * P * PACK], BF16, name="z_grouped%d%d" % (q, g), align_bytes=64)
-                    regroup(nc.vector.tensor_copy, grouped[:], z_planes[:, g * PACK : (g + 1) * PACK, half_tokens(q)])
-                    z_grouped[q, g] = grouped
+            def regroup_z(q, g):
+                by_vector(z_grouped[:, q, g, :], z_planes[:, g * PACK : (g + 1) * PACK, half(q)])
 
             def quantise_z(q):
-                for g in range(PASSES):
-                    quantise_unit(z_grouped[q, g], z, g, half_tokens(q))
+                nc.vector.quantize_mx(
+                    out=z_codes[:, q].rearrange("p g n -> p (g n)").bitcast(FP8X4),
+                    scales=z_scales[:, q].rearrange("p g n -> p (g n)"),
+                    in_=z_grouped[:, q].rearrange("p g x -> p (g x)"),
+                )
 
-            copy_wo(0, 0, N_TILE // 2)
+            copy_wo(by_both(N_TILE // 2), 0, 0)
             for m in range(TOK_TILES):
                 turn_h(m)
                 quantise_h(m)
             quantise_wo(0, 0)
-            copy_wo(0, 1, BY_SCALAR)
-            copy_wo(1, 0, BY_VECTOR)
-            copy_wo(1, 1, N_TILE // 2)
+            copy_wo(by_scalar, 0, 1)
+            copy_wo(by_vector, 1, 0)
+            copy_wo(by_both(N_TILE // 2), 1, 1)
             quantise_wo(0, 1)
             quantise_wo(1, 0)
             quantise_wo(1, 1)
             load_gain()
             project(0)
             project(1)
-            unit(GATE, 0, 0, BY_SCALAR)
+            unit(by_scalar, GATE, 0, 0)
+            shared_unit_by_gpsimd(0)
             statistics(0)
-            row_scalars(0)
-            gpsimd_share(GATE, 0, 1)
             statistics(1)
-            row_shift(0)
-            unit(GATE, 1, 0, BY_SCALAR)
+            row_scales(0)
+            statistics(2)
+            row_shifts(0)
+            statistics(3)
+            row_scales(1)
+            unit(by_scalar, GATE, 1, 0)
             normalise(0)
             normalise(1)
-            row_scalars(1)
-            unit(GATE, 0, 1, BY_VECTOR, True)
-            row_shift(1)
-            quantise_weight_tile(GATE, 0)
-            flip(0, range(0))
-            unit(UP, 0, 0, BY_SCALAR)
-            unit(GATE, 1, 1, BY_VECTOR)
-            unit(UP, 0, 1, BY_VECTOR)
+            shared_unit_by_vector(0)
+            quantise_tile(GATE, 0)
+            row_shifts(1)
             normalise(2)
             normalise(3)
-            flip(1, range(0))
-            regroup_z(0)
-            quantise_weight_tile(GATE, 1)
+            shared_unit_by_gpsimd(1)
+            flip(0, range(E_BLOCKS))
+            regroup_z(0, 0)
+            regroup_z(0, 1)
+            shared_unit_by_vector(1)
+            flip(1, ())
             quantise_z(0)
-            unit(UP, 1, 0, BY_SCALAR)
-            quantise_weight_tile(UP, 0)
-            regroup_z(1)
-            unit(UP, 1, 1, BY_VECTOR)
-            load_chunks(RAW_BUFS + 4)
+            unit(by_scalar, UP, 0, 0)
+            unit(by_vector, UP, 0, 1)
+            regroup_z(1, 0)
+            regroup_z(1, 1)
+            quantise_tile(GATE, 1)
             quantise_z(1)
-
+            unit(by_scalar, UP, 1, 0)
+            quantise_tile(UP, 0)
+            load_chunks(RAW_BUFS + 3)
+            unit(by_vector, UP, 1, 1)
+            load_chunks(RAW_BUFS + 4)
 
         late = ctx.enter_context(tc.tile_pool(name="late", bufs=1, reuse_waits="tile"))
         gates = {}
 
+        def branch(b, j, m):
+            acc = bank([P, N_TILE], F32)
+            q, cols = m // 2, slice(m % 2 * P, (m % 2 + 1) * P)
+            codes, scales = moving[b, j]
+            for g in range(PASSES):
+                product(acc[:], (z_codes[:, q, g, cols], z_scales[:, q, g, cols]), (codes[:, g, :], scales[:, g, :]), g)
+            return acc
+
         def gate_branch(j):
             for m in range(TOK_TILES):
-                acc = bank([P, N_TILE], F32)
-                for g in range(PASSES):
-                    product(acc[:], z, tokens(m), moving[GATE, j], slice(0, N_TILE), g)
+                acc = branch(GATE, j, m)
                 gates[j, m] = late.tile([P, N_TILE], F32, name="gate", bufs=2 * TOK_TILES)
                 nc.scalar.activation(out=gates[j, m][:], in_=acc[:], func=ACT.Gelu)
 
         def up_branch(j):
             for m in range(TOK_TILES):
-                acc = bank([P, N_TILE], F32)
-                for g in range(PASSES):
-                    product(acc[:], z, tokens(m), moving[UP, j], slice(0, N_TILE), g)
+                acc = branch(UP, j, m)
                 result = late.tile([P, N_TILE], F32, name="result", bufs=2 * TOK_TILES)
                 nc.vector.tensor_tensor(out=result[:], in0=gates[j, m][:], in1=acc[:], op=ALU.mult)
                 nc.sync.dma_start(out=out[m, :, j * N_TILE : (j + 1) * N_TILE], in_=result[:])
 
-        engines = {}
-        for j in range(2, F_TILES):
-            engines[GATE, j, 0] = BY_SCALAR
-            engines[GATE, j, 1] = BY_VECTOR
-            engines[UP, j, 0] = BY_SCALAR
-            engines[UP, j, 1] = BY_VECTOR
-
-        def copy_tile(j):
-            for b in (GATE, UP):
-                for g in range(PASSES):
-                    if (b, g) != (UP, 1) or j < FIRST_SHARED_TILE:
-                        unit(b, j, g, engines[b, j, g])
-                        if j % TILES_PER_CHUNK == TILES_PER_CHUNK - 1:
-                            load_chunks(RAW_BUFS + 4 * (j // TILES_PER_CHUNK) + 2 * b + g + 1)
+        def last_use(b, j, g):
+            if j % TILES_PER_CHUNK == TILES_PER_CHUNK - 1:
+                load_chunks(RAW_BUFS + load_order.index((b, j // TILES_PER_CHUNK, g)) + 1)
 
         gate_branch(0)
-        copy_tile(2)
-        quantise_weight_tile(UP, 1)
+        unit(by_scalar, GATE, 2, 0)
         for j in range(F_TILES):
             up_branch(j)
-            if FIRST_SHARED_TILE <= j + 2 < F_TILES:
-                gpsimd_share(UP, j + 2, 1)
-                unit(UP, j + 2, 1, engines[UP, j + 2, 1], True)
-                if j % TILES_PER_CHUNK == TILES_PER_CHUNK - 1:
-                    load_chunks(RAW_BUFS + 4 * ((j + 2) // TILES_PER_CHUNK) + 4)
+            if j + 2 < F_TILES:
+                shared_unit_by_gpsimd(j + 2)
             if j + 1 < F_TILES:
                 gate_branch(j + 1)
-            if j + 3 < F_TILES:
-                copy_tile(j + 3)
+                quantise_tile(UP, j + 1)
             if j + 2 < F_TILES:
-                quantise_weight_tile(GATE, j + 2)
-                quantise_weight_tile(UP, j + 2)
+                shared_unit_by_vector(j + 2)
+                last_use(GATE, j + 2, 1)
+                unit(by_both(VECTOR_COLS) if VECTOR_COLS else by_scalar, UP, j + 2, 0)
+                unit(by_vector, UP, j + 2, 1)
+                last_use(UP, j + 2, 1)
+            if j + 3 < F_TILES:
+                unit(by_scalar, GATE, j + 3, 0)
+            if j + 2 < F_TILES:
+                quantise_tile(GATE, j + 2)

@@ -161,9 +161,9 @@ def tile_selfdecoderblock_pb_kernel(tc, h_attn, Wo, gamma2, beta2, Wg, Wu, out):
 
         ident_f32 = keep.tile([P, P], F32, name="ident_f32")
         make_identity(nc, ident_f32[:])
-        zero = keep.tile([P, 1], F32, name="zero")
-        nc.vector.memset(zero[:], 0.0)
-        warm = keep.tile([P, 1], F32, name="warm")
+        eps = keep.tile([P, 1], F32, name="eps")
+        nc.vector.memset(eps[:], EPS)
+        warm = keep.tile([P, 2], F32, name="warm")
         z_codes = keep.tile([P, HALVES, PASSES, HALF], U32, name="z_codes", align_bytes=64)
         z_scales = keep.tile([P, HALVES, PASSES, HALF], U8, name="z_scales", align_bytes=64)
 
@@ -193,7 +193,7 @@ def tile_selfdecoderblock_pb_kernel(tc, h_attn, Wo, gamma2, beta2, Wg, Wu, out):
                     out=gb_rows[:, i, :, 0:PACK], in_=vec.rearrange("(g p t) -> p g t", g=PASSES, t=PACK)
                 )
             load_chunks(RAW_BUFS)
-            nc.scalar.activation(out=warm[:], in_=zero[:], func=ACT.Gelu)
+            nc.scalar.activation(out=warm[:, 0:1], in_=eps[:], func=ACT.Sqrt)
 
             wo_codes = early.tile([P, PASSES, E], U32, name="wo_codes", align_bytes=64)
             wo_scales = early.tile([P, PASSES, E], U8, name="wo_scales", align_bytes=64)
@@ -253,9 +253,7 @@ def tile_selfdecoderblock_pb_kernel(tc, h_attn, Wo, gamma2, beta2, Wg, Wu, out):
 
             stats = early.tile([P, TOK_TILES, TILES_PER_CHUNK, 6], F32, name="stats")
             mean_var = early.tile([P, TOK_TILES, 2], F32, name="mean_var")
-            spread = early.tile([P, TOK_TILES], F32, name="spread")
-            minus_half = early.tile([P, TOK_TILES], F32, name="minus_half")
-            nc.gpsimd.memset(minus_half[:], -0.5)
+            std = early.tile([P, TOK_TILES], F32, name="std")
             rstd = early.tile([P, TOK_TILES], F32, name="rstd")
             shift = early.tile([P, TOK_TILES], F32, name="shift")
             normed = {}
@@ -273,15 +271,16 @@ def tile_selfdecoderblock_pb_kernel(tc, h_attn, Wo, gamma2, beta2, Wg, Wu, out):
                     nc.vector.bn_stats(out=stats[:, m, n, :], in_=a[m, n][:])
                 nc.vector.bn_aggr(out=mean_var[:, m, :], in_=stats[:, m].rearrange("p n s -> p (n s)"))
 
-            def row_scales(q):
+            def row_roots(q):
                 pair = slice(2 * q, 2 * q + 2)
-                nc.gpsimd.tensor_scalar(
-                    out=spread[:, pair], in0=mean_var[:, pair, 1], scalar1=1.0, scalar2=EPS, op0=ALU.mult, op1=ALU.add
-                )
-                nc.gpsimd.tensor_tensor(out=rstd[:, pair], in0=spread[:, pair], in1=minus_half[:, pair], op=ALU.pow)
+                nc.scalar.activation(out=std[:, pair], in_=mean_var[:, pair, 1], func=ACT.Sqrt, bias=eps[:], scale=1.0)
+
+            def load_gelu():
+                nc.scalar.activation(out=warm[:, 1:2], in_=std[:, TOK_TILES - 1 : TOK_TILES], func=ACT.Gelu)
 
             def row_shifts(q):
                 pair = slice(2 * q, 2 * q + 2)
+                nc.vector.reciprocal(out=rstd[:, pair], in_=std[:, pair])
                 nc.vector.scalar_tensor_tensor(
                     out=shift[:, pair],
                     in0=mean_var[:, pair, 0],
@@ -366,17 +365,18 @@ def tile_selfdecoderblock_pb_kernel(tc, h_attn, Wo, gamma2, beta2, Wg, Wu, out):
             shared_unit_by_gpsimd(0)
             statistics(0)
             statistics(1)
-            row_scales(0)
+            unit(by_scalar, GATE, 1, 0)
+            row_roots(0)
             statistics(2)
             row_shifts(0)
             statistics(3)
-            row_scales(1)
-            unit(by_scalar, GATE, 1, 0)
             normalise(0)
+            row_roots(1)
+            load_gelu()
             normalise(1)
             shared_unit_by_vector(0)
-            quantise_tile(GATE, 0)
             row_shifts(1)
+            quantise_tile(GATE, 0)
             normalise(2)
             normalise(3)
             shared_unit_by_gpsimd(1)

@@ -34,8 +34,7 @@ GB_PITCH = 16
 RAW_BUFS = 8
 GATE = 0
 UP = 1
-GPSIMD_COLS = 384
-VECTOR_COLS = 64
+VECTOR_COLS = 128
 
 FLOPS = 2 * TOKENS * E * (E + 2 * F)
 
@@ -120,43 +119,27 @@ def tile_selfdecoderblock_pb_kernel(tc, h_attn, Wo, gamma2, beta2, Wg, Wu, out):
             start = (j % TILES_PER_CHUNK) * N_TILE
             return raws[b, j // TILES_PER_CHUNK, g][:, :, start : start + N_TILE]
 
+        def pair(name):
+            return stage.tile([P, PASSES, UNIT], BF16, name=name, bufs=3 if name == "up" else 1, align_bytes=64)
+
+        NAMES = {(GATE, 0): "first", (UP, 0): "gate", (UP, 7): "gate"}
+
+        def grouped_unit(b, j, g):
+            if (b, j) not in grouped_units:
+                grouped_units[b, j] = pair(NAMES.get((b, j), "gate" if b == GATE else "up"))
+            return grouped_units[b, j][:, g, :]
+
         def unit(copy, b, j, g):
-            if b == UP:
-                if g == 0:
-                    grouped_units[b, j] = stage.tile(
-                        [P, PASSES, UNIT], BF16, name="pair", bufs=3, align_bytes=64
-                    )
-                grouped = grouped_units[b, j][:, g, :]
-            else:
-                tile = stage.tile([P, UNIT], BF16, name="single", bufs=6, align_bytes=64)
-                grouped_units[b, j, g] = tile
-                grouped = tile[:]
-            copy(grouped, raw_unit(b, j, g))
-
-        def shared_unit_by_gpsimd(j):
-            tile = stage.tile([P, UNIT], BF16, name="shared", bufs=1, align_bytes=64)
-            grouped_units[GATE, j, 1] = tile
-            cut = N_TILE - GPSIMD_COLS
-            by_gpsimd(tile[:, cut * PACK :], raw_unit(GATE, j, 1)[:, :, cut:])
-
-        def shared_unit_by_vector(j):
-            cut = N_TILE - GPSIMD_COLS
-            by_vector(grouped_units[GATE, j, 1][:, 0 : cut * PACK], raw_unit(GATE, j, 1)[:, :, 0:cut])
+            copy(grouped_unit(b, j, g), raw_unit(b, j, g))
 
         def quantise_tile(b, j):
             codes = weights.tile([P, PASSES, N_TILE], U32, name="codes", align_bytes=64)
             scales = weights.tile([P, PASSES, N_TILE], U8, name="scales", align_bytes=64)
-            if b == UP:
-                nc.vector.quantize_mx(
-                    out=codes[:].rearrange("p g n -> p (g n)").bitcast(FP8X4),
-                    scales=scales[:].rearrange("p g n -> p (g n)"),
-                    in_=grouped_units[b, j][:].rearrange("p g x -> p (g x)"),
-                )
-            else:
-                for g in range(PASSES):
-                    nc.vector.quantize_mx(
-                        out=codes[:, g, :].bitcast(FP8X4), scales=scales[:, g, :], in_=grouped_units[b, j, g][:]
-                    )
+            nc.vector.quantize_mx(
+                out=codes[:].rearrange("p g n -> p (g n)").bitcast(FP8X4),
+                scales=scales[:].rearrange("p g n -> p (g n)"),
+                in_=grouped_units[b, j][:].rearrange("p g x -> p (g x)"),
+            )
             moving[b, j] = (codes, scales)
 
         ident_f32 = keep.tile([P, P], F32, name="ident_f32")
@@ -176,17 +159,19 @@ def tile_selfdecoderblock_pb_kernel(tc, h_attn, Wo, gamma2, beta2, Wg, Wu, out):
                 load_rows(raw[:], wo_dram, g, n * N_TILE, N_TILE)
                 wo_raw[g, n] = raw
 
-            def load_h():
-                for m in range(TOK_TILES):
-                    rows = early.tile([P, E], BF16, name="h_rows%d" % m)
-                    nc.sync.dma_start(out=rows[:], in_=h_rows_dram[m])
-                    h_rows.append(rows)
+            def load_h(m):
+                rows = early.tile([P, E], BF16, name="h_rows%d" % m)
+                nc.sync.dma_start(out=rows[:], in_=h_rows_dram[m])
+                h_rows.append(rows)
 
             load_wo(0, 0)
-            load_h()
             load_wo(0, 1)
             load_wo(1, 0)
             load_wo(1, 1)
+            load_h(0)
+            load_h(1)
+            load_h(2)
+            load_h(3)
             gb_rows = early.tile([P, 2, PASSES, GB_PITCH], BF16, name="gb_rows")
             for i, vec in enumerate((gamma2, beta2)):
                 nc.sync.dma_start(
@@ -200,14 +185,14 @@ def tile_selfdecoderblock_pb_kernel(tc, h_attn, Wo, gamma2, beta2, Wg, Wu, out):
             wo_grouped = {}
 
             def copy_wo(copy, g, n):
-                grouped = stage.tile([P, UNIT], BF16, name="single", bufs=6, align_bytes=64)
-                copy(grouped[:], wo_raw[g, n][:])
-                wo_grouped[g, n] = grouped
+                if n == 0:
+                    wo_grouped[g] = pair("up" if g == 0 else "first")
+                copy(wo_grouped[g][:, n, :], wo_raw[g, n][:])
 
             def quantise_wo(g, n):
                 cols = slice(n * N_TILE, (n + 1) * N_TILE)
                 nc.vector.quantize_mx(
-                    out=wo_codes[:, g, cols].bitcast(FP8X4), scales=wo_scales[:, g, cols], in_=wo_grouped[g, n][:]
+                    out=wo_codes[:, g, cols].bitcast(FP8X4), scales=wo_scales[:, g, cols], in_=wo_grouped[g][:, n, :]
                 )
 
             h_codes = early.tile([P, TOK_TILES, PASSES, P], U32, name="h_codes", align_bytes=64)
@@ -348,55 +333,59 @@ def tile_selfdecoderblock_pb_kernel(tc, h_attn, Wo, gamma2, beta2, Wg, Wu, out):
                 )
 
             copy_wo(by_both(N_TILE // 2), 0, 0)
-            for m in range(TOK_TILES):
-                turn_h(m)
-                quantise_h(m)
+            copy_wo(by_both(N_TILE // 2), 0, 1)
             quantise_wo(0, 0)
-            copy_wo(by_scalar, 0, 1)
-            copy_wo(by_vector, 1, 0)
-            copy_wo(by_both(N_TILE // 2), 1, 1)
+            copy_wo(by_both(N_TILE // 2), 1, 0)
             quantise_wo(0, 1)
+            copy_wo(by_both(N_TILE // 2), 1, 1)
             quantise_wo(1, 0)
+            turn_h(0)
+            quantise_h(0)
+            turn_h(1)
+            quantise_h(1)
+            turn_h(2)
+            turn_h(3)
             quantise_wo(1, 1)
+            quantise_h(2)
+            quantise_h(3)
             load_gain()
             project(0)
             project(1)
-            unit(by_scalar, GATE, 0, 0)
-            shared_unit_by_gpsimd(0)
+            unit(by_gpsimd, GATE, 0, 0)
+            unit(by_gpsimd, GATE, 0, 1)
+            unit(by_scalar, GATE, 1, 0)
+            unit(by_scalar, GATE, 1, 1)
             statistics(0)
             statistics(1)
-            unit(by_scalar, GATE, 1, 0)
             row_roots(0)
+            unit(by_scalar, UP, 1, 0)
             statistics(2)
-            row_shifts(0)
             statistics(3)
-            normalise(0)
+            row_shifts(0)
             row_roots(1)
-            load_gelu()
+            normalise(0)
             normalise(1)
-            shared_unit_by_vector(0)
-            row_shifts(1)
             quantise_tile(GATE, 0)
+            row_shifts(1)
+            unit(by_vector, UP, 1, 1)
+            quantise_tile(GATE, 1)
             normalise(2)
             normalise(3)
-            shared_unit_by_gpsimd(1)
+            unit(by_gpsimd, UP, 0, 1)
             flip(0, range(E_BLOCKS))
             regroup_z(0, 0)
             regroup_z(0, 1)
-            shared_unit_by_vector(1)
-            flip(1, ())
             quantise_z(0)
-            unit(by_scalar, UP, 0, 0)
-            unit(by_vector, UP, 0, 1)
+            flip(1, ())
+            load_gelu()
+            load_chunks(RAW_BUFS + 2)
+            unit(by_both(N_TILE // 2), UP, 0, 0)
+            load_chunks(RAW_BUFS + 4)
             regroup_z(1, 0)
             regroup_z(1, 1)
-            quantise_tile(GATE, 1)
             quantise_z(1)
-            unit(by_scalar, UP, 1, 0)
             quantise_tile(UP, 0)
-            load_chunks(RAW_BUFS + 3)
-            unit(by_vector, UP, 1, 1)
-            load_chunks(RAW_BUFS + 4)
+            quantise_tile(UP, 1)
 
         late = ctx.enter_context(tc.tile_pool(name="late", bufs=1, reuse_waits="tile"))
         gates = {}
@@ -409,39 +398,48 @@ def tile_selfdecoderblock_pb_kernel(tc, h_attn, Wo, gamma2, beta2, Wg, Wu, out):
                 product(acc[:], (z_codes[:, q, g, cols], z_scales[:, q, g, cols]), (codes[:, g, :], scales[:, g, :]), g)
             return acc
 
+        def gate_product(j, m):
+            acc = branch(GATE, j, m)
+            gates[j, m] = late.tile([P, N_TILE], F32, name="gate", bufs=2 * TOK_TILES)
+            nc.scalar.activation(out=gates[j, m][:], in_=acc[:], func=ACT.Gelu)
+
+        def up_product(j, m):
+            acc = branch(UP, j, m)
+            result = late.tile([P, N_TILE], F32, name="result", bufs=2 * TOK_TILES)
+            nc.vector.tensor_tensor(out=result[:], in0=gates[j, m][:], in1=acc[:], op=ALU.mult)
+            nc.sync.dma_start(out=out[m, :, j * N_TILE : (j + 1) * N_TILE], in_=result[:])
+
         def gate_branch(j):
             for m in range(TOK_TILES):
-                acc = branch(GATE, j, m)
-                gates[j, m] = late.tile([P, N_TILE], F32, name="gate", bufs=2 * TOK_TILES)
-                nc.scalar.activation(out=gates[j, m][:], in_=acc[:], func=ACT.Gelu)
+                gate_product(j, m)
 
         def up_branch(j):
             for m in range(TOK_TILES):
-                acc = branch(UP, j, m)
-                result = late.tile([P, N_TILE], F32, name="result", bufs=2 * TOK_TILES)
-                nc.vector.tensor_tensor(out=result[:], in0=gates[j, m][:], in1=acc[:], op=ALU.mult)
-                nc.sync.dma_start(out=out[m, :, j * N_TILE : (j + 1) * N_TILE], in_=result[:])
+                up_product(j, m)
 
         def last_use(b, j, g):
             if j % TILES_PER_CHUNK == TILES_PER_CHUNK - 1:
                 load_chunks(RAW_BUFS + load_order.index((b, j // TILES_PER_CHUNK, g)) + 1)
 
         gate_branch(0)
-        unit(by_scalar, GATE, 2, 0)
-        for j in range(F_TILES):
+        for j in range(F_TILES - 1):
             up_branch(j)
             if j + 2 < F_TILES:
-                shared_unit_by_gpsimd(j + 2)
-            if j + 1 < F_TILES:
-                gate_branch(j + 1)
-                quantise_tile(UP, j + 1)
-            if j + 2 < F_TILES:
-                shared_unit_by_vector(j + 2)
+                unit(by_gpsimd, GATE, j + 2, 1)
+                unit(by_scalar, GATE, j + 2, 0)
                 last_use(GATE, j + 2, 1)
-                unit(by_both(VECTOR_COLS) if VECTOR_COLS else by_scalar, UP, j + 2, 0)
+                gate_branch(j + 1)
+                if j > 0:
+                    quantise_tile(UP, j + 1)
+            if j + 3 < F_TILES:
+                unit(by_both(VECTOR_COLS), UP, j + 2, 0)
                 unit(by_vector, UP, j + 2, 1)
                 last_use(UP, j + 2, 1)
-            if j + 3 < F_TILES:
-                unit(by_scalar, GATE, j + 3, 0)
             if j + 2 < F_TILES:
                 quantise_tile(GATE, j + 2)
+        last = F_TILES - 1
+        unit(by_gpsimd, UP, last, 1)
+        unit(by_scalar, UP, last, 0)
+        gate_branch(last)
+        quantise_tile(UP, last)
+        up_branch(last)

@@ -32,9 +32,11 @@ RUN_S = 4
 EPS = 1e-6
 GB_PITCH = 16
 RAW_BUFS = 8
+CHUNK_PARTS = 2 * PASSES
+GPSIMD_COLS = 384
 GATE = 0
 UP = 1
-VECTOR_COLS = 128
+VECTOR_COLS = 64
 
 FLOPS = 2 * TOKENS * E * (E + 2 * F)
 
@@ -132,14 +134,24 @@ def tile_selfdecoderblock_pb_kernel(tc, h_attn, Wo, gamma2, beta2, Wg, Wu, out):
         def unit(copy, b, j, g):
             copy(grouped_unit(b, j, g), raw_unit(b, j, g))
 
-        def quantise_tile(b, j):
+        def columns(copy, b, j, g, first, end):
+            copy(grouped_unit(b, j, g)[:, first * PACK : end * PACK], raw_unit(b, j, g)[:, :, first:end])
+
+        def gpsimd_part(b, j, g):
+            columns(by_gpsimd, b, j, g, N_TILE - GPSIMD_COLS, N_TILE)
+
+        def vector_part(b, j, g):
+            columns(by_vector, b, j, g, 0, N_TILE - GPSIMD_COLS)
+
+        def quantise_tile(b, j, by_passes=False):
             codes = weights.tile([P, PASSES, N_TILE], U32, name="codes", align_bytes=64)
             scales = weights.tile([P, PASSES, N_TILE], U8, name="scales", align_bytes=64)
-            nc.vector.quantize_mx(
-                out=codes[:].rearrange("p g n -> p (g n)").bitcast(FP8X4),
-                scales=scales[:].rearrange("p g n -> p (g n)"),
-                in_=grouped_units[b, j][:].rearrange("p g x -> p (g x)"),
-            )
+            for span in [slice(g, g + 1) for g in range(PASSES)] if by_passes else [slice(0, PASSES)]:
+                nc.vector.quantize_mx(
+                    out=codes[:, span].rearrange("p g n -> p (g n)").bitcast(FP8X4),
+                    scales=scales[:, span].rearrange("p g n -> p (g n)"),
+                    in_=grouped_units[b, j][:, span].rearrange("p g x -> p (g x)"),
+                )
             moving[b, j] = (codes, scales)
 
         ident_f32 = keep.tile([P, P], F32, name="ident_f32")
@@ -172,6 +184,7 @@ def tile_selfdecoderblock_pb_kernel(tc, h_attn, Wo, gamma2, beta2, Wg, Wu, out):
             load_h(1)
             load_h(2)
             load_h(3)
+            load_chunks(PASSES)
             gb_rows = early.tile([P, 2, PASSES, GB_PITCH], BF16, name="gb_rows")
             for i, vec in enumerate((gamma2, beta2)):
                 nc.sync.dma_start(
@@ -254,6 +267,10 @@ def tile_selfdecoderblock_pb_kernel(tc, h_attn, Wo, gamma2, beta2, Wg, Wu, out):
             def statistics(m):
                 for n in range(TILES_PER_CHUNK):
                     nc.vector.bn_stats(out=stats[:, m, n, :], in_=a[m, n][:])
+                    if n == 0 and m > 0:
+                        join_statistics(m - 1)
+
+            def join_statistics(m):
                 nc.vector.bn_aggr(out=mean_var[:, m, :], in_=stats[:, m].rearrange("p n s -> p (n s)"))
 
             def row_roots(q):
@@ -348,38 +365,41 @@ def tile_selfdecoderblock_pb_kernel(tc, h_attn, Wo, gamma2, beta2, Wg, Wu, out):
             quantise_wo(1, 1)
             quantise_h(2)
             quantise_h(3)
-            load_gain()
             project(0)
             project(1)
             unit(by_gpsimd, GATE, 0, 0)
-            unit(by_gpsimd, GATE, 0, 1)
+            gpsimd_part(GATE, 0, 1)
             unit(by_scalar, GATE, 1, 0)
-            unit(by_scalar, GATE, 1, 1)
             statistics(0)
             statistics(1)
-            row_roots(0)
-            unit(by_scalar, UP, 1, 0)
             statistics(2)
+            row_roots(0)
+            unit(by_scalar, GATE, 1, 1)
             statistics(3)
+            join_statistics(3)
             row_shifts(0)
             row_roots(1)
             normalise(0)
             normalise(1)
-            quantise_tile(GATE, 0)
+            vector_part(GATE, 0, 1)
             row_shifts(1)
-            unit(by_vector, UP, 1, 1)
+            quantise_tile(GATE, 0)
+            load_gain()
             quantise_tile(GATE, 1)
             normalise(2)
             normalise(3)
-            unit(by_gpsimd, UP, 0, 1)
+            gpsimd_part(UP, 0, 1)
             flip(0, range(E_BLOCKS))
+            unit(by_scalar, UP, 1, 0)
             regroup_z(0, 0)
             regroup_z(0, 1)
+            unit(by_vector, UP, 1, 1)
             quantise_z(0)
             flip(1, ())
-            load_gelu()
             load_chunks(RAW_BUFS + 2)
             unit(by_both(N_TILE // 2), UP, 0, 0)
+            vector_part(UP, 0, 1)
+            load_gelu()
             load_chunks(RAW_BUFS + 4)
             regroup_z(1, 0)
             regroup_z(1, 1)
@@ -390,12 +410,15 @@ def tile_selfdecoderblock_pb_kernel(tc, h_attn, Wo, gamma2, beta2, Wg, Wu, out):
         late = ctx.enter_context(tc.tile_pool(name="late", bufs=1, reuse_waits="tile"))
         gates = {}
 
-        def branch(b, j, m):
-            acc = bank([P, N_TILE], F32)
+        def add_passes(acc, b, j, m, passes):
             q, cols = m // 2, slice(m % 2 * P, (m % 2 + 1) * P)
             codes, scales = moving[b, j]
-            for g in range(PASSES):
+            for g in passes:
                 product(acc[:], (z_codes[:, q, g, cols], z_scales[:, q, g, cols]), (codes[:, g, :], scales[:, g, :]), g)
+
+        def branch(b, j, m):
+            acc = bank([P, N_TILE], F32)
+            add_passes(acc, b, j, m, range(PASSES))
             return acc
 
         def gate_product(j, m):
@@ -403,11 +426,15 @@ def tile_selfdecoderblock_pb_kernel(tc, h_attn, Wo, gamma2, beta2, Wg, Wu, out):
             gates[j, m] = late.tile([P, N_TILE], F32, name="gate", bufs=2 * TOK_TILES)
             nc.scalar.activation(out=gates[j, m][:], in_=acc[:], func=ACT.Gelu)
 
-        def up_product(j, m):
-            acc = branch(UP, j, m)
+        def up_product(j, m, acc):
             result = late.tile([P, N_TILE], F32, name="result", bufs=2 * TOK_TILES)
-            nc.vector.tensor_tensor(out=result[:], in0=gates[j, m][:], in1=acc[:], op=ALU.mult)
-            nc.sync.dma_start(out=out[m, :, j * N_TILE : (j + 1) * N_TILE], in_=result[:])
+            pieces = 2 if (j, m) == (F_TILES - 1, TOK_TILES - 1) else 1
+            for first in range(0, N_TILE, N_TILE // pieces):
+                cols = slice(first, first + N_TILE // pieces)
+                nc.vector.tensor_tensor(out=result[:, cols], in0=gates[j, m][:, cols], in1=acc[:, cols], op=ALU.mult)
+                nc.sync.dma_start(
+                    out=out[m, :, j * N_TILE + first : j * N_TILE + first + N_TILE // pieces], in_=result[:, cols]
+                )
 
         def gate_branch(j):
             for m in range(TOK_TILES):
@@ -415,31 +442,37 @@ def tile_selfdecoderblock_pb_kernel(tc, h_attn, Wo, gamma2, beta2, Wg, Wu, out):
 
         def up_branch(j):
             for m in range(TOK_TILES):
-                up_product(j, m)
+                up_product(j, m, branch(UP, j, m))
 
-        def last_use(b, j, g):
+        def last_use(j):
             if j % TILES_PER_CHUNK == TILES_PER_CHUNK - 1:
-                load_chunks(RAW_BUFS + load_order.index((b, j // TILES_PER_CHUNK, g)) + 1)
+                load_chunks(RAW_BUFS + CHUNK_PARTS * (j // TILES_PER_CHUNK + 1))
 
         gate_branch(0)
         for j in range(F_TILES - 1):
             up_branch(j)
             if j + 2 < F_TILES:
-                unit(by_gpsimd, GATE, j + 2, 1)
+                gpsimd_part(GATE, j + 2, 1)
                 unit(by_scalar, GATE, j + 2, 0)
-                last_use(GATE, j + 2, 1)
                 gate_branch(j + 1)
                 if j > 0:
                     quantise_tile(UP, j + 1)
+                vector_part(GATE, j + 2, 1)
             if j + 3 < F_TILES:
                 unit(by_both(VECTOR_COLS), UP, j + 2, 0)
                 unit(by_vector, UP, j + 2, 1)
-                last_use(UP, j + 2, 1)
             if j + 2 < F_TILES:
+                last_use(j + 2)
                 quantise_tile(GATE, j + 2)
         last = F_TILES - 1
-        unit(by_gpsimd, UP, last, 1)
-        unit(by_scalar, UP, last, 0)
+        gpsimd_part(UP, last, 1)
+        unit(by_both(VECTOR_COLS), UP, last, 0)
         gate_branch(last)
-        quantise_tile(UP, last)
-        up_branch(last)
+        vector_part(UP, last, 1)
+        quantise_tile(UP, last, by_passes=True)
+        accs = [bank([P, N_TILE], F32), bank([P, N_TILE], F32)]
+        for g in range(PASSES):
+            for m in range(2):
+                add_passes(accs[m], UP, last, m, [g])
+        for m in range(TOK_TILES):
+            up_product(last, m, accs[m] if m < 2 else branch(UP, last, m))

from contextlib import ExitStack

import concourse.mybir as mybir
from concourse.masks import make_identity

F32 = mybir.dt.float32
BF16 = mybir.dt.bfloat16
U32 = mybir.dt.uint32
U8 = mybir.dt.uint8
FP8X4 = mybir.dt.float8_e4m3fn_x4
ACT = mybir.ActivationFunctionType
ALU = mybir.AluOpType

P = 128
PACK = 4
K_PASS = P * PACK
TOKENS = 512
TOK_TILES = TOKENS // P
HALVES = 2
HALF = TOKENS // HALVES
E = 1024
F = 4096
PASSES = E // K_PASS
N_TILE = 512
UNIT = N_TILE * PACK
CHUNK = 1024
TILES_PER_CHUNK = CHUNK // N_TILE
F_TILES = F // N_TILE
E_BLOCKS = E // P
RUN_V = 4
RUN_S = 4
EPS = 1e-6
GB_PITCH = 16
RAW_BUFS = 8
CHUNK_PARTS = 2 * PASSES
GPSIMD_COLS = 384
GATE = 0
UP = 1
VECTOR_COLS = 64

FLOPS = 2 * TOKENS * E * (E + 2 * F)


def regroup(copy, grouped, rows, run):
    copy(
        out=grouped.rearrange("p (c i t) -> p c t i", i=run, t=PACK),
        in_=rows.rearrange("p t (c i) -> p c t i", i=run),
    )


def tile_selfdecoderblock_pb_kernel(tc, h_attn, Wo, gamma2, beta2, Wg, Wu, out):
    nc = tc.nc
    h_rows_dram = h_attn.rearrange("b s h d -> b s (h d)")
    wo_dram = Wo.rearrange("h d e -> (h d) e")
    load_order = [(b, c, g) for c in range(F // CHUNK) for b in (GATE, UP) for g in range(PASSES)]

    with ExitStack() as ctx:
        ctx.enter_context(tc.manual_schedule())
        keep = ctx.enter_context(tc.tile_pool(name="keep", bufs=1))
        raw_pool = ctx.enter_context(tc.tile_pool(name="raw", bufs=RAW_BUFS))
        stage = ctx.enter_context(tc.tile_pool(name="stage", bufs=1))
        weights = ctx.enter_context(tc.tile_pool(name="weights", bufs=6))
        psum = ctx.enter_context(tc.psum_pool(name="psum", bufs=8))

        def bank(shape, dtype):
            return psum.tile(shape, dtype, name="bank")

        def load_rows(raw, w, g, first, width):
            nc.sync.dma_start(
                out=raw,
                in_=w[g * K_PASS : (g + 1) * K_PASS, first : first + width].rearrange("(p t) n -> p t n", t=PACK),
            )

        raws = {}

        def load_chunks(count):
            for b, c, g in load_order[len(raws) : count]:
                raw = raw_pool.tile([P, PACK, CHUNK], BF16, name="raw")
                load_rows(raw[:], (Wg, Wu)[b], g, c * CHUNK, CHUNK)
                raws[b, c, g] = raw

        def product(acc, left, right, g):
            nc.tensor.matmul_mx(
                out=acc,
                lhsT=left[0].bitcast(FP8X4),
                lhsT_scale=left[1],
                rhs=right[0].bitcast(FP8X4),
                rhs_scale=right[1],
                start=(g == 0),
                stop=(g == PASSES - 1),
            )

        def by_scalar(grouped, rows):
            regroup(nc.scalar.copy, grouped, rows, RUN_S)

        def by_vector(grouped, rows):
            regroup(nc.vector.tensor_copy, grouped, rows, RUN_V)

        def by_both(cols):
            def copy(grouped, rows):
                cut = N_TILE - cols
                by_scalar(grouped[:, 0 : cut * PACK], rows[:, :, 0:cut])
                by_vector(grouped[:, cut * PACK :], rows[:, :, cut:])

            return copy

        def by_gpsimd(grouped, rows):
            nc.gpsimd.tensor_scalar(
                out=grouped.rearrange("p (c t) -> p c t", t=PACK),
                in0=rows.rearrange("p t c -> p c t"),
                scalar1=1.0,
                scalar2=0.0,
                op0=ALU.mult,
                op1=ALU.add,
            )

        grouped_units = {}
        moving = {}

        def raw_unit(b, j, g):
            start = (j % TILES_PER_CHUNK) * N_TILE
            return raws[b, j // TILES_PER_CHUNK, g][:, :, start : start + N_TILE]

        def pair(name):
            return stage.tile([P, PASSES, UNIT], BF16, name=name, bufs=3 if name == "up" else 1, align_bytes=64)

        NAMES = {(GATE, 0): "first", (UP, 0): "gate", (UP, 7): "gate"}

        def grouped_unit(b, j, g):
            if (b, j) not in grouped_units:
                grouped_units[b, j] = pair(NAMES.get((b, j), "gate" if b == GATE else "up"))
            return grouped_units[b, j][:, g, :]

        def unit(copy, b, j, g):
            copy(grouped_unit(b, j, g), raw_unit(b, j, g))

        def columns(copy, b, j, g, first, end):
            copy(grouped_unit(b, j, g)[:, first * PACK : end * PACK], raw_unit(b, j, g)[:, :, first:end])

        def gpsimd_part(b, j, g):
            columns(by_gpsimd, b, j, g, N_TILE - GPSIMD_COLS, N_TILE)

        def vector_part(b, j, g):
            columns(by_vector, b, j, g, 0, N_TILE - GPSIMD_COLS)

        def quantise_tile(b, j, by_passes=False):
            codes = weights.tile([P, PASSES, N_TILE], U32, name="codes", align_bytes=64)
            scales = weights.tile([P, PASSES, N_TILE], U8, name="scales", align_bytes=64)
            for span in [slice(g, g + 1) for g in range(PASSES)] if by_passes else [slice(0, PASSES)]:
                nc.vector.quantize_mx(
                    out=codes[:, span].rearrange("p g n -> p (g n)").bitcast(FP8X4),
                    scales=scales[:, span].rearrange("p g n -> p (g n)"),
                    in_=grouped_units[b, j][:, span].rearrange("p g x -> p (g x)"),
                )
            moving[b, j] = (codes, scales)

        ident_f32 = keep.tile([P, P], F32, name="ident_f32")
        make_identity(nc, ident_f32[:])
        eps = keep.tile([P, 1], F32, name="eps")
        nc.vector.memset(eps[:], EPS)
        warm = keep.tile([P, 2], F32, name="warm")
        z_codes = keep.tile([P, HALVES, PASSES, HALF], U32, name="z_codes", align_bytes=64)
        z_scales = keep.tile([P, HALVES, PASSES, HALF], U8, name="z_scales", align_bytes=64)

        with tc.tile_pool(name="early", bufs=1) as early:
            wo_raw = {}
            h_rows = []

            def load_wo(g, n):
                raw = early.tile([P, PACK, N_TILE], BF16, name="wide", bufs=4)
                load_rows(raw[:], wo_dram, g, n * N_TILE, N_TILE)
                wo_raw[g, n] = raw

            def load_h(m):
                rows = early.tile([P, E], BF16, name="h_rows%d" % m)
                nc.sync.dma_start(out=rows[:], in_=h_rows_dram[m])
                h_rows.append(rows)

            load_wo(0, 0)
            load_wo(0, 1)
            load_wo(1, 0)
            load_wo(1, 1)
            load_h(0)
            load_h(1)
            load_h(2)
            load_h(3)
            load_chunks(PASSES)
            gb_rows = early.tile([P, 2, PASSES, GB_PITCH], BF16, name="gb_rows")
            for i, vec in enumerate((gamma2, beta2)):
                nc.sync.dma_start(
                    out=gb_rows[:, i, :, 0:PACK], in_=vec.rearrange("(g p t) -> p g t", g=PASSES, t=PACK)
                )
            load_chunks(RAW_BUFS)
            nc.scalar.activation(out=warm[:, 0:1], in_=eps[:], func=ACT.Sqrt)

            wo_codes = early.tile([P, PASSES, E], U32, name="wo_codes", align_bytes=64)
            wo_scales = early.tile([P, PASSES, E], U8, name="wo_scales", align_bytes=64)
            wo_grouped = {}

            def copy_wo(copy, g, n):
                if n == 0:
                    wo_grouped[g] = pair("up" if g == 0 else "first")
                copy(wo_grouped[g][:, n, :], wo_raw[g, n][:])

            def quantise_wo(g, n):
                cols = slice(n * N_TILE, (n + 1) * N_TILE)
                nc.vector.quantize_mx(
                    out=wo_codes[:, g, cols].bitcast(FP8X4), scales=wo_scales[:, g, cols], in_=wo_grouped[g][:, n, :]
                )

            h_codes = early.tile([P, TOK_TILES, PASSES, P], U32, name="h_codes", align_bytes=64)
            h_scales = early.tile([P, TOK_TILES, PASSES, P], U8, name="h_scales", align_bytes=64)
            h_grouped = []

            def turn_h(m):
                words = bank([P, PASSES * 2, P], F32)
                for q in range(PASSES * 2):
                    first = (q // 2) * 2 * P + q % 2
                    nc.tensor.transpose(
                        words[:, q, :], h_rows[m][:].bitcast(F32)[:, first : (q // 2 + 1) * 2 * P : 2], ident_f32[:]
                    )
                grouped = early.tile([P, PASSES, P * PACK], BF16, name="h_grouped%d" % m, align_bytes=64)
                nc.scalar.copy(
                    out=grouped[:].bitcast(F32).rearrange("p g (r u) -> p g r u", u=2),
                    in_=words[:].rearrange("p (g u) r -> p g r u", u=2),
                )
                h_grouped.append(grouped)

            def quantise_h(m):
                nc.vector.quantize_mx(
                    out=h_codes[:, m].rearrange("p g n -> p (g n)").bitcast(FP8X4),
                    scales=h_scales[:, m].rearrange("p g n -> p (g n)"),
                    in_=h_grouped[m][:].rearrange("p g x -> p (g x)"),
                )

            a = {}

            def project(q):
                for g in range(PASSES):
                    for n in range(TILES_PER_CHUNK):
                        cols = slice(n * N_TILE, (n + 1) * N_TILE)
                        for m in (2 * q, 2 * q + 1):
                            if g == 0:
                                a[m, n] = bank([P, N_TILE], F32)
                            product(
                                a[m, n][:],
                                (h_codes[:, m, g, :], h_scales[:, m, g, :]),
                                (wo_codes[:, g, cols], wo_scales[:, g, cols]),
                                g,
                            )

            stats = early.tile([P, TOK_TILES, TILES_PER_CHUNK, 6], F32, name="stats")
            mean_var = early.tile([P, TOK_TILES, 2], F32, name="mean_var")
            std = early.tile([P, TOK_TILES], F32, name="std")
            rstd = early.tile([P, TOK_TILES], F32, name="rstd")
            shift = early.tile([P, TOK_TILES], F32, name="shift")
            normed = {}
            gain_bias = early.tile([P, 2 * E_BLOCKS], F32, name="gain_bias")
            z_planes = early.tile([P, E_BLOCKS, TOKENS], BF16, name="z_planes")
            z_grouped = early.tile([P, HALVES, PASSES, HALF * PACK], BF16, name="z_grouped", align_bytes=64)

            def load_gain():
                nc.vector.tensor_copy(
                    out=gain_bias[:].rearrange("p (i g t) -> p i g t", i=2, t=PACK), in_=gb_rows[:, :, :, 0:PACK]
                )

            def statistics(m):
                for n in range(TILES_PER_CHUNK):
                    nc.vector.bn_stats(out=stats[:, m, n, :], in_=a[m, n][:])
                    if n == 0 and m > 0:
                        join_statistics(m - 1)

            def join_statistics(m):
                nc.vector.bn_aggr(out=mean_var[:, m, :], in_=stats[:, m].rearrange("p n s -> p (n s)"))

            def row_roots(q):
                pair = slice(2 * q, 2 * q + 2)
                nc.scalar.activation(out=std[:, pair], in_=mean_var[:, pair, 1], func=ACT.Sqrt, bias=eps[:], scale=1.0)

            def load_gelu():
                nc.scalar.activation(out=warm[:, 1:2], in_=std[:, TOK_TILES - 1 : TOK_TILES], func=ACT.Gelu)

            def row_shifts(q):
                pair = slice(2 * q, 2 * q + 2)
                nc.vector.reciprocal(out=rstd[:, pair], in_=std[:, pair])
                nc.vector.scalar_tensor_tensor(
                    out=shift[:, pair],
                    in0=mean_var[:, pair, 0],
                    scalar=-1.0,
                    in1=rstd[:, pair],
                    op0=ALU.mult,
                    op1=ALU.mult,
                )

            def normalise(m):
                normed[m] = early.tile([P, E], F32, name="wide", bufs=4)
                for n in range(TILES_PER_CHUNK):
                    nc.scalar.activation(
                        out=normed[m][:, n * N_TILE : (n + 1) * N_TILE].rearrange("p (t q) -> p t q", t=PACK),
                        in_=a[m, n][:].rearrange("p (q t) -> p t q", t=PACK),
                        func=ACT.Identity,
                        scale=rstd[:, m : m + 1],
                        bias=shift[:, m : m + 1],
                    )

            def half(q):
                return slice(q * HALF, (q + 1) * HALF)

            def flip(q, vector_blocks):
                for first_block in range(0, E_BLOCKS, 2):
                    flipped = bank([P, 2, HALF], F32)
                    for i in range(2):
                        r = first_block + i
                        for s in range(2):
                            nc.tensor.transpose(
                                flipped[:, i, s * P : (s + 1) * P],
                                normed[2 * q + s][:, r * P : (r + 1) * P],
                                ident_f32[:],
                            )
                    for i in range(2):
                        r = first_block + i
                        gain = gain_bias[:, r : r + 1]
                        bias = gain_bias[:, E_BLOCKS + r : E_BLOCKS + r + 1]
                        if r in vector_blocks:
                            nc.vector.tensor_scalar(
                                out=z_planes[:, r, half(q)],
                                in0=flipped[:, i, :],
                                scalar1=gain,
                                scalar2=bias,
                                op0=ALU.mult,
                                op1=ALU.add,
                            )
                        else:
                            nc.scalar.activation(
                                out=z_planes[:, r, half(q)],
                                in_=flipped[:, i, :],
                                func=ACT.Identity,
                                scale=gain,
                                bias=bias,
                            )

            def regroup_z(q, g):
                by_vector(z_grouped[:, q, g, :], z_planes[:, g * PACK : (g + 1) * PACK, half(q)])

            def quantise_z(q):
                nc.vector.quantize_mx(
                    out=z_codes[:, q].rearrange("p g n -> p (g n)").bitcast(FP8X4),
                    scales=z_scales[:, q].rearrange("p g n -> p (g n)"),
                    in_=z_grouped[:, q].rearrange("p g x -> p (g x)"),
                )

            copy_wo(by_both(N_TILE // 2), 0, 0)
            copy_wo(by_both(N_TILE // 2), 0, 1)
            quantise_wo(0, 0)
            copy_wo(by_both(N_TILE // 2), 1, 0)
            quantise_wo(0, 1)
            copy_wo(by_both(N_TILE // 2), 1, 1)
            quantise_wo(1, 0)
            turn_h(0)
            quantise_h(0)
            turn_h(1)
            quantise_h(1)
            turn_h(2)
            turn_h(3)
            quantise_wo(1, 1)
            quantise_h(2)
            quantise_h(3)
            project(0)
            project(1)
            unit(by_gpsimd, GATE, 0, 0)
            gpsimd_part(GATE, 0, 1)
            unit(by_scalar, GATE, 1, 0)
            statistics(0)
            statistics(1)
            statistics(2)
            row_roots(0)
            unit(by_scalar, GATE, 1, 1)
            statistics(3)
            join_statistics(3)
            row_shifts(0)
            row_roots(1)
            normalise(0)
            normalise(1)
            vector_part(GATE, 0, 1)
            row_shifts(1)
            quantise_tile(GATE, 0)
            load_gain()
            quantise_tile(GATE, 1)
            normalise(2)
            normalise(3)
            gpsimd_part(UP, 0, 1)
            flip(0, range(E_BLOCKS))
            unit(by_scalar, UP, 1, 0)
            regroup_z(0, 0)
            regroup_z(0, 1)
            unit(by_vector, UP, 1, 1)
            quantise_z(0)
            flip(1, ())
            load_chunks(RAW_BUFS + 2)
            unit(by_both(N_TILE // 2), UP, 0, 0)
            vector_part(UP, 0, 1)
            load_gelu()
            load_chunks(RAW_BUFS + 4)
            regroup_z(1, 0)
            regroup_z(1, 1)
            quantise_z(1)
            quantise_tile(UP, 0)
            quantise_tile(UP, 1)

        late = ctx.enter_context(tc.tile_pool(name="late", bufs=1, reuse_waits="tile"))
        gates = {}

        def add_passes(acc, b, j, m, passes):
            q, cols = m // 2, slice(m % 2 * P, (m % 2 + 1) * P)
            codes, scales = moving[b, j]
            for g in passes:
                product(acc[:], (z_codes[:, q, g, cols], z_scales[:, q, g, cols]), (codes[:, g, :], scales[:, g, :]), g)

        def branch(b, j, m):
            acc = bank([P, N_TILE], F32)
            add_passes(acc, b, j, m, range(PASSES))
            return acc

        def gate_product(j, m):
            acc = branch(GATE, j, m)
            gates[j, m] = late.tile([P, N_TILE], F32, name="gate", bufs=2 * TOK_TILES)
            nc.scalar.activation(out=gates[j, m][:], in_=acc[:], func=ACT.Gelu)

        def up_product(j, m, acc):
            result = late.tile([P, N_TILE], F32, name="result", bufs=2 * TOK_TILES)
            pieces = 2 if (j, m) == (F_TILES - 1, TOK_TILES - 1) else 1
            for first in range(0, N_TILE, N_TILE // pieces):
                cols = slice(first, first + N_TILE // pieces)
                nc.vector.tensor_tensor(out=result[:, cols], in0=gates[j, m][:, cols], in1=acc[:, cols], op=ALU.mult)
                nc.sync.dma_start(
                    out=out[m, :, j * N_TILE + first : j * N_TILE + first + N_TILE // pieces], in_=result[:, cols]
                )

        def gate_branch(j):
            for m in range(TOK_TILES):
                gate_product(j, m)

        def up_branch(j):
            for m in range(TOK_TILES):
                up_product(j, m, branch(UP, j, m))

        def last_use(j):
            if j % TILES_PER_CHUNK == TILES_PER_CHUNK - 1:
                load_chunks(RAW_BUFS + CHUNK_PARTS * (j // TILES_PER_CHUNK + 1))

        gate_branch(0)
        for j in range(F_TILES - 1):
            up_branch(j)
            if j + 2 < F_TILES:
                gpsimd_part(GATE, j + 2, 1)
                unit(by_scalar, GATE, j + 2, 0)
                gate_branch(j + 1)
                if j > 0:
                    quantise_tile(UP, j + 1)
                vector_part(GATE, j + 2, 1)
            if j + 3 < F_TILES:
                unit(by_both(VECTOR_COLS), UP, j + 2, 0)
                unit(by_vector, UP, j + 2, 1)
            if j + 2 < F_TILES:
                last_use(j + 2)
                quantise_tile(GATE, j + 2)
        last = F_TILES - 1
        gpsimd_part(UP, last, 1)
        unit(by_both(VECTOR_COLS), UP, last, 0)
        gate_branch(last)
        vector_part(UP, last, 1)
        quantise_tile(UP, last, by_passes=True)
        accs = [bank([P, N_TILE], F32), bank([P, N_TILE], F32)]
        for g in range(PASSES):
            for m in range(2):
                add_passes(accs[m], UP, last, m, [g])
        for m in range(TOK_TILES):
            up_product(last, m, accs[m] if m < 2 else branch(UP, last, m))
